import numpy as np
import ml_dtypes


def mxq(x, axis, fmt="e4m3"):
    dtype, down = {"e4m3": (ml_dtypes.float8_e4m3fn, 7), "e5m2": (ml_dtypes.float8_e5m2, 14)}[fmt]
    v = np.moveaxis(np.asarray(x, np.float32).astype(ml_dtypes.bfloat16).astype(np.float64), axis, -1)
    blocks = v.reshape(v.shape[:-1] + (-1, 32))
    amax = np.abs(blocks).max(-1, keepdims=True)
    byte = np.maximum(np.where(amax > 0, np.frexp(amax)[1] - 1 + 127, 0) - down, 1)
    scale = np.exp2(byte - 127.0)
    codes = (blocks / scale).astype(np.float32).astype(dtype).astype(np.float64)
    return np.moveaxis((codes * scale).reshape(v.shape), -1, axis)


WIDE = False


def mx_kscale(k):
    if not WIDE:
        return np.ones(k)
    levels = np.array([10, -10, 5, -5, 0])
    if k % 512:
        return np.exp2(np.random.permutation(np.resize(levels, k // 32))).repeat(32)
    a = np.empty((k // 512, 16))
    for p in range(k // 512):
        a[p, :8] = np.random.permutation(np.resize(levels, 8))
        for g in range(8):
            far = levels[np.abs(levels - a[p, g]) >= 10]
            a[p, g + 8] = far[np.random.randint(len(far))]
    return np.exp2(a.ravel()).repeat(32)


BF16 = ml_dtypes.bfloat16


def bf(x):
    return np.asarray(x, np.float32).astype(BF16)


def f64(x):
    return np.asarray(x).astype(np.float64)


B, L, H, G, DEPTH = 64, 64, 1024, 256, 3
EPS = 1e-5


def layernorm(v, g, b):
    mu = v.mean(-1, keepdims=True)
    var = np.square(v - mu).mean(-1, keepdims=True)
    return (v - mu) / np.sqrt(var + EPS) * g + b


def draw0():
    s, t = mx_kscale(H), mx_kscale(H)
    return {"x_nodes": bf(np.random.standard_normal((B, L, H)) * s),
            "w1": bf(np.random.standard_normal((H, H)) / np.sqrt(H) / s[:, None]),
            "b1": bf(np.random.standard_normal(H) * 0.3),
            "gamma": bf((1.0 + 0.1 * np.random.standard_normal(H)) * t),
            "beta": bf(0.2 * np.random.standard_normal(H) * t),
            "w2": bf(np.random.standard_normal((H, G)) / np.sqrt(H) / t[:, None]),
            "b2": bf(np.random.standard_normal(G) * 0.3)}


def core(x_nodes, w1, b1, gamma, beta, w2, b2):
    h = (mxq(f64(x_nodes), 2, "e4m3") @ mxq(f64(w1), 0, "e4m3")) + f64(b1)
    r = np.maximum(layernorm(h, f64(gamma), f64(beta)), 0.0)
    x1 = (mxq(r, 2, "e4m3") @ mxq(f64(w2), 0, "e4m3")) + f64(b2)
    x2 = np.broadcast_to(x1.max(axis=1, keepdims=True), x1.shape)
    return np.concatenate([x1, x2], axis=2)


def e4m3fn_bytes(y):
    return np.clip(np.asarray(y, np.float64), -448.0, 448.0).astype(np.float32).astype(ml_dtypes.float8_e4m3fn).view(np.uint8)


def e4m3fn_values(b):
    return np.asarray(b, np.uint8).view(ml_dtypes.float8_e4m3fn).astype(np.float64)


def setup_inputs():
    d = draw0()
    x0 = np.asarray(d['x_nodes']).astype(np.float64)
    s = (np.max(np.abs(x0), axis=(0, 1), keepdims=True) / 448.0).astype(np.float32)
    out = {}
    for k, v in d.items():
        if k == 'x_nodes':
            out['x_nodes_bytes'] = e4m3fn_bytes(x0 / s.astype(np.float64))
            out['x_nodes_scale'] = s
        else:
            out[k] = v
    return out


def reference(x_nodes_bytes, x_nodes_scale, w1, b1, gamma, beta, w2, b2):
    return core(e4m3fn_values(x_nodes_bytes) * x_nodes_scale.astype(np.float64), w1, b1, gamma, beta, w2, b2)

@@ -1,0 +1,566 @@
+from contextlib import ExitStack
+
+import concourse.mybir as mybir
+from concourse.masks import make_identity
+
+B, L, H, G = 64, 64, 1024, 256
+EPS = 1e-5
+BF16_MAX = 3.3895313892515355e38
+FLOPS = 2 * B * L * H * (H + G)
+
+F32 = mybir.dt.float32
+BF16 = mybir.dt.bfloat16
+U32 = mybir.dt.uint32
+U8 = mybir.dt.uint8
+FP8 = mybir.dt.float8_e4m3fn
+FP8X4 = mybir.dt.float8_e4m3fn_x4
+ALU = mybir.AluOpType
+ACT = mybir.ActivationFunctionType
+
+P = 128
+PACK = 4
+K_PASS = P * PACK
+PASSES = H // K_PASS
+BANK = 512
+TILES_PER_GROUP = 4
+GROUP = P * TILES_PER_GROUP
+GROUPS = B * L // GROUP
+TILES = GROUPS * TILES_PER_GROUP
+HALVES = G // P
+POLYS = GROUP // L
+ROWS_PER_POLY = P // POLYS
+N_LAG = 6
+X_LEAD = 5
+Y_SHIFT = 20
+A_SHIFT = -4
+T_SHIFT = 20
+V_NORM = 1
+M2 = 7
+TAIL_SHARE = 320
+A_LATE = 1
+H_BANKS = 3
+POOL_SHARE = 256
+SCALAR_SHARE = 0
+
+
+def tile_sub_graph_pa_t_kernel(tc, x_bytes, x_scale, w1, b1, gamma, beta, w2, b2, out):
+    nc = tc.nc
+    x_rows = x_bytes.rearrange("b l h -> (b l) h").rearrange("(k p j) h -> k p j h", p=P, j=TILES_PER_GROUP)
+    out_rows = out.rearrange("b l c -> (b l) c").rearrange("(k p j) c -> k p j c", p=P, j=TILES_PER_GROUP)
+
+    with ExitStack() as ctx:
+        keep = ctx.enter_context(tc.tile_pool(name="keep", bufs=1))
+        work = ctx.enter_context(tc.tile_pool(name="work", bufs=2))
+        psum = ctx.enter_context(tc.psum_pool(name="psum", bufs=1))
+        ctx.enter_context(tc.manual_schedule())
+
+        ident = keep.tile([P, P], F32)
+        make_identity(nc, ident[:])
+
+        scale_col = keep.tile([P, PASSES, PACK], F32)
+        nc.sync.dma_start(out=scale_col[:], in_=x_scale.rearrange("a b (g p t) -> p (a b g) t", p=P, t=PACK))
+        xb = {}
+
+        def load_x(first, count):
+            k, j = divmod(first, TILES_PER_GROUP)
+            rows = keep.tile([P, count, H], U8, name="xbytes%d" % first)
+            nc.sync.dma_start(out=rows[:], in_=x_rows[k, :, j : j + count, :])
+            for n in range(count):
+                xb[first + n] = rows[:, n, :]
+
+        w1_raw = {}
+
+        def load_w1(g, c):
+            w1_raw[g, c] = keep.tile([P, PACK, BANK], BF16, name="w1raw%d%d" % (g, c))
+            rows = w1[g * K_PASS : (g + 1) * K_PASS, c * BANK : (c + 1) * BANK]
+            nc.sync.dma_start(out=w1_raw[g, c][:], in_=rows.rearrange("(p j) n -> p j n", j=PACK))
+
+        load_x(0, 2)
+        load_w1(0, 0)
+        load_w1(1, 0)
+        load_x(2, 2)
+        load_w1(0, 1)
+        load_w1(1, 1)
+        b1_raw = keep.tile([P, H], BF16)
+        nc.sync.dma_start(out=b1_raw[:], in_=b1.partition_broadcast(P))
+        load_x(4, 4)
+        gamma_raw = keep.tile([P, PASSES, PACK], BF16)
+        nc.sync.dma_start(out=gamma_raw[:], in_=gamma.rearrange("(g p t) -> p g t", p=P, t=PACK))
+        beta_raw = keep.tile([P, PASSES, PACK], BF16)
+        nc.sync.dma_start(out=beta_raw[:], in_=beta.rearrange("(g p t) -> p g t", p=P, t=PACK))
+        w2_raw = keep.tile([P, PASSES, PACK, G], BF16)
+        nc.sync.dma_start(
+            out=w2_raw[:].rearrange("p g j n -> p g (j n)"),
+            in_=w2.rearrange("(g p j) n -> p g (j n)", p=P, j=PACK),
+        )
+        b2_raw = keep.tile([P, HALVES, 2], BF16)
+        with nc.allow_non_contiguous_dma(reason="one bias value to a partition and half"):
+            nc.sync.dma_start(out=b2_raw[:, :, 0], in_=b2.rearrange("(h p) -> p h", p=P))
+        for k in range(2, GROUPS):
+            load_x(k * TILES_PER_GROUP, TILES_PER_GROUP)
+
+        scale_row = []
+        for g in range(PASSES):
+            bank = psum.tile([P, P, PACK], F32, name="scale%d" % g)
+            for t in range(PACK):
+                nc.tensor.transpose(bank[:, :, t], scale_col[:, g, t : t + 1].to_broadcast([P, P]), ident[:])
+            scale_row.append(bank)
+
+        w1_codes, w1_scales, w1_grouped = {}, {}, {}
+
+        def group_w1(g, c, engine_copy):
+            w1_grouped[g, c] = keep.tile([P, PACK, P, PACK], BF16, name="w1grp%d%d" % (g, c), align_bytes=64)
+            engine_copy(
+                out=w1_grouped[g, c][:].rearrange("p t (a i) j -> p a t i j", i=2),
+                in_=w1_raw[g, c][:].rearrange("p j (a i t) -> p a t i j", i=2, t=PACK),
+            )
+
+        def quantize_w1(g, c):
+            w1_codes[g, c] = keep.tile([P, BANK], U32, name="w1codes%d%d" % (g, c), align_bytes=64)
+            w1_scales[g, c] = keep.tile([P, BANK], U8, name="w1scales%d%d" % (g, c), align_bytes=64)
+            nc.vector.quantize_mx(
+                out=w1_codes[g, c][:].bitcast(FP8X4),
+                scales=w1_scales[g, c][:],
+                in_=w1_grouped[g, c][:].rearrange("p t m j -> p (t m j)"),
+            )
+
+        b1_row = keep.tile([P, PASSES, PACK, P], F32)
+        gamma_col = keep.tile([P, PASSES, PACK], F32)
+        beta_col = keep.tile([P, PASSES, PACK], F32)
+        b2_col = keep.tile([P, HALVES], F32)
+        w2_grouped = keep.tile([P, PASSES, G, PACK], BF16, align_bytes=64)
+        w2_codes = keep.tile([P, PASSES, G], U32, align_bytes=64)
+        w2_scales = keep.tile([P, PASSES, G], U8, align_bytes=64)
+
+        def prepare_b1():
+            nc.scalar.copy(out=b1_row[:], in_=b1_raw[:].rearrange("p (c m t) -> p c t m", c=PASSES, t=PACK))
+
+        def prepare_columns():
+            nc.scalar.copy(out=gamma_col[:], in_=gamma_raw[:])
+            nc.scalar.copy(out=beta_col[:], in_=beta_raw[:])
+            nc.scalar.copy(out=b2_col[:], in_=b2_raw[:, :, 0])
+
+        def group_w2():
+            for g in range(PASSES):
+                nc.scalar.copy(
+                    out=w2_grouped[:, g, :, :].rearrange("p (a i) j -> p a j i", i=4),
+                    in_=w2_raw[:, g, :, :].rearrange("p j (a i) -> p a j i", i=4),
+                )
+
+        def quantize_w2():
+            nc.vector.quantize_mx(
+                out=w2_codes[:].rearrange("p g n -> p (g n)").bitcast(FP8X4),
+                scales=w2_scales[:].rearrange("p g n -> p (g n)"),
+                in_=w2_grouped[:].rearrange("p g n j -> p (g n j)"),
+            )
+
+        xw, xt, xg, xq, xs = {}, {}, {}, {}, {}
+        h_ps, hb, sums, negmu, ssq, std, rstd, nrm = {}, {}, {}, {}, {}, {}, {}, {}
+
+        def scale_x(i, g):
+            k, j = divmod(i, TILES_PER_GROUP)
+            if g == 0:
+                xw[i] = work.tile([P, H], BF16, name="xw", bufs=3)
+            cols = slice(g * K_PASS, (g + 1) * K_PASS)
+            nc.vector.tensor_tensor(
+                out=xw[i][:, cols],
+                in0=xb[i][:, cols].bitcast(FP8),
+                in1=scale_row[g][:].rearrange("p m t -> p (m t)"),
+                op=ALU.mult,
+            )
+
+        def turn_x(i):
+            xt[i] = psum.tile([P, PASSES, 2, P], F32, name="ring", bufs=6 - H_BANKS)
+            words = xw[i][:].bitcast(F32)
+            for g in range(PASSES):
+                for u in range(2):
+                    nc.tensor.transpose(xt[i][:, g, u, :], words[:, 2 * P * g + u : 2 * P * (g + 1) : 2], ident[:])
+
+        def copy_x(i):
+            pair, n = divmod(i, 2)
+            if n == 0:
+                xg[pair] = work.tile([P, 2, H], BF16, name="xg", bufs=2, align_bytes=64)
+            nc.scalar.copy(
+                out=xg[pair][:, n, :].bitcast(F32).rearrange("p (g r u) -> p g r u", g=PASSES, u=2),
+                in_=xt[i][:].rearrange("p g u r -> p g r u"),
+            )
+
+        def quantize_x(i):
+            pair = i // 2
+            codes = work.tile([P, 2, PASSES, P], U32, name="xq", bufs=3, align_bytes=64)
+            scales = work.tile([P, 2, PASSES, P], U8, name="xs", bufs=3, align_bytes=64)
+            nc.vector.quantize_mx(
+                out=codes[:].rearrange("p n g r -> p (n g r)").bitcast(FP8X4),
+                scales=scales[:].rearrange("p n g r -> p (n g r)"),
+                in_=xg[pair][:].rearrange("p n c -> p (n c)"),
+            )
+            for n in range(2):
+                xq[2 * pair + n] = codes[:, n, :, :]
+                xs[2 * pair + n] = scales[:, n, :, :]
+
+        def matmul1(i, c):
+            h_ps[i, c] = psum.tile([P, BANK], F32, name="hps", bufs=H_BANKS)
+            for g in range(PASSES):
+                nc.tensor.matmul_mx(
+                    out=h_ps[i, c][:],
+                    lhsT=xq[i][:, g, :].bitcast(FP8X4),
+                    lhsT_scale=xs[i][:, g, :],
+                    rhs=w1_codes[g, c][:].bitcast(FP8X4),
+                    rhs_scale=w1_scales[g, c][:],
+                    start=(g == 0),
+                    stop=(g == PASSES - 1),
+                )
+
+        def add_bias(i):
+            hb[i] = work.tile([P, PASSES, BANK], F32, name="hb", bufs=4)
+            sums[i] = work.tile([P, PASSES], F32, name="sums", bufs=3)
+            for c in range(PASSES):
+                nc.vector.scalar_tensor_tensor(
+                    out=hb[i][:, c, :],
+                    in0=h_ps[i, c][:],
+                    scalar=1.0,
+                    in1=b1_row[:, c, :, :].rearrange("p t m -> p (t m)"),
+                    op0=ALU.mult,
+                    op1=ALU.add,
+                    accum_out=sums[i][:, c : c + 1],
+                )
+
+        def mean(i):
+            negmu[i] = work.tile([P, 1], F32, name="negmu", bufs=4)
+            nc.vector.tensor_scalar(
+                out=negmu[i][:],
+                in0=sums[i][:, 0:1],
+                scalar1=sums[i][:, 1:2],
+                scalar2=-1.0 / H,
+                op0=ALU.add,
+                op1=ALU.mult,
+            )
+
+        def variance(i):
+            squares = work.tile([P, H], BF16, name="squares", bufs=2)
+            ssq[i] = work.tile([P, 1], F32, name="ssq", bufs=3)
+            nc.scalar.activation(
+                out=squares[:],
+                in_=hb[i][:].rearrange("p c n -> p (c n)"),
+                func=ACT.Square,
+                bias=negmu[i][:],
+                accum_out=ssq[i][:],
+            )
+
+        def deviation(i):
+            std[i] = work.tile([P, 1], F32, name="std", bufs=3)
+            nc.scalar.activation(out=std[i][:], in_=ssq[i][:], func=ACT.Sqrt, scale=1.0 / H, bias=EPS)
+
+        def inverse(i):
+            rstd[i] = work.tile([P, 1], F32, name="rstd", bufs=3)
+            nc.vector.reciprocal(out=rstd[i][:], in_=std[i][:])
+
+        def normalize(i, engine):
+            nrm[i] = work.tile([P, H], F32, name="nrm", bufs=8)
+            engine.tensor_scalar(
+                out=nrm[i][:],
+                in0=hb[i][:].rearrange("p c n -> p (c n)"),
+                scalar1=negmu[i][:],
+                scalar2=rstd[i][:],
+                op0=ALU.add,
+                op1=ALU.mult,
+            )
+
+        nt, planes, rg, rq, rs = {}, {}, {}, {}, {}
+        y_ps, y, pooled, spread, yt, own, shared = {}, {}, {}, {}, {}, {}, {}
+
+        def turn_n(k, c, on_vector):
+            if on_vector:
+                nt[k, c] = psum.tile([P, TILES_PER_GROUP, P], F32, name="scale%d" % (c // 2 % 2))
+            else:
+                nt[k, c] = psum.tile([P, TILES_PER_GROUP, P], F32, name="ring", bufs=6 - H_BANKS)
+            for j in range(TILES_PER_GROUP):
+                nc.tensor.transpose(nt[k, c][:, j, :], nrm[k * TILES_PER_GROUP + j][:, c * P : (c + 1) * P], ident[:])
+
+        def affine_relu(k, c, on_vector):
+            g, t = divmod(c, PACK)
+            if t == 0:
+                planes[k, g] = work.tile([P, PACK, GROUP], BF16, name="planes", bufs=3)
+            turned = nt[k, c][:].rearrange("p j r -> p (j r)")
+            if on_vector:
+                nc.vector.tensor_scalar(
+                    out=planes[k, g][:, t, :],
+                    in0=turned,
+                    scalar1=gamma_col[:, g, t : t + 1],
+                    scalar2=beta_col[:, g, t : t + 1],
+                    op0=ALU.mult,
+                    op1=ALU.add,
+                )
+            else:
+                nc.scalar.activation(
+                    out=planes[k, g][:, t, :],
+                    in_=turned,
+                    func=ACT.Relu,
+                    scale=gamma_col[:, g, t : t + 1],
+                    bias=beta_col[:, g, t : t + 1],
+                )
+
+        def group_r(k, g, engine, first, last):
+            if first == last:
+                return
+            if (k, g) not in rg:
+                rg[k, g] = work.tile([P, GROUP, PACK], BF16, name="rg", bufs=2, align_bytes=64)
+            dst = rg[k, g][:, first:last, :].rearrange("p (a i) t -> p a t i", i=4)
+            src = planes[k, g][:, :, first:last].rearrange("p t (a i) -> p a t i", i=4)
+            if engine is nc.scalar:
+                nc.scalar.copy(out=dst, in_=src)
+            else:
+                engine.tensor_scalar(out=dst, in0=src, scalar1=BF16_MAX, scalar2=0.0, op0=ALU.min, op1=ALU.max)
+
+        def quantize_r(k, g):
+            rq[k, g] = work.tile([P, GROUP], U32, name="rq", bufs=3, align_bytes=64)
+            rs[k, g] = work.tile([P, GROUP], U8, name="rs", bufs=3, align_bytes=64)
+            nc.vector.quantize_mx(
+                out=rq[k, g][:].bitcast(FP8X4),
+                scales=rs[k, g][:],
+                in_=rg[k, g][:].rearrange("p n t -> p (n t)"),
+            )
+
+        def matmul2(k, h, bank="ring"):
+            y_ps[k, h] = psum.tile([P, GROUP], F32, name=bank, bufs=3)
+            for g in range(PASSES):
+                nc.tensor.matmul_mx(
+                    out=y_ps[k, h][:],
+                    lhsT=w2_codes[:, g, h * P : (h + 1) * P].bitcast(FP8X4),
+                    lhsT_scale=w2_scales[:, g, h * P : (h + 1) * P],
+                    rhs=rq[k, g][:].bitcast(FP8X4),
+                    rhs_scale=rs[k, g][:],
+                    start=(g == 0),
+                    stop=(g == PASSES - 1),
+                )
+
+        def add_bias2(k, h, on_vector):
+            y[k, h] = work.tile([P, GROUP], F32, name="y", bufs=4)
+            if on_vector:
+                nc.vector.tensor_scalar(
+                    out=y[k, h][:], in0=y_ps[k, h][:], scalar1=b2_col[:, h : h + 1], scalar2=None, op0=ALU.add
+                )
+            else:
+                nc.scalar.activation(out=y[k, h][:], in_=y_ps[k, h][:], func=ACT.Identity, bias=b2_col[:, h : h + 1])
+
+        def pool_nodes(k, h):
+            if h == 0:
+                pooled[k] = work.tile([P, HALVES * POLYS, 1], F32, name="pooled", bufs=2)
+            nc.vector.tensor_reduce(
+                out=pooled[k][:, h * POLYS : (h + 1) * POLYS, 0],
+                in_=y[k, h][:].rearrange("p (j b q) -> p b j q", j=TILES_PER_GROUP, b=POLYS),
+                axis=mybir.AxisListType.XY,
+                op=ALU.max,
+            )
+
+        def spread_pooled(k):
+            spread[k] = work.tile([P, HALVES * POLYS, ROWS_PER_POLY], F32, name="spread", bufs=2)
+            nc.vector.tensor_copy(
+                out=spread[k][:], in_=pooled[k][:].to_broadcast([P, HALVES * POLYS, ROWS_PER_POLY])
+            )
+
+        def turn_y(k, pair, bank="ring"):
+            yt[k, pair] = psum.tile([P, 2, G], F32, name=bank, bufs=3)
+            for jj in range(2):
+                j = 2 * pair + jj
+                for h in range(HALVES):
+                    nc.tensor.transpose(
+                        yt[k, pair][:, jj, h * P : (h + 1) * P], y[k, h][:, j * P : (j + 1) * P], ident[:]
+                    )
+
+        def store_own(k, pair, engine_copy):
+            own[k, pair] = work.tile([P, 2, G], F32, name="own", bufs=4)
+            engine_copy(out=own[k, pair][:], in_=yt[k, pair][:])
+            nc.sync.dma_start(out=out_rows[k, :, 2 * pair : 2 * pair + 2, 0:G], in_=own[k, pair][:])
+
+        def turn_pooled(k, bank="ring"):
+            yt[k, 2] = psum.tile([P, 1, G], F32, name=bank, bufs=3)
+            flat = spread[k][:].rearrange("p a q -> p (a q)")
+            for h in range(HALVES):
+                nc.tensor.transpose(yt[k, 2][:, 0, h * P : (h + 1) * P], flat[:, h * P : (h + 1) * P], ident[:])
+
+        def store_pooled(k, engine_copy):
+            shared[k] = work.tile([P, 1, G], F32, name="shared", bufs=2)
+            engine_copy(out=shared[k][:], in_=yt[k, 2][:])
+            nc.sync.dma_start(
+                out=out_rows[k, :, :, G : 2 * G], in_=shared[k][:].to_broadcast([P, TILES_PER_GROUP, G])
+            )
+
+        def on_tile(stage, i, *args):
+            if 0 <= i < TILES:
+                stage(i, *args)
+
+        def on_group(stage, s, lag, *args):
+            k, rest = divmod(s - lag, TILES_PER_GROUP)
+            if rest == 0 and 0 <= k < GROUPS:
+                stage(k, *args)
+
+        def on_plane(stage, n, *args):
+            k, c = divmod(n, PASSES * PACK)
+            if 0 <= k < GROUPS:
+                stage(k, c, *args)
+
+        def prepare_x(i):
+            scale_x(i, 0)
+            scale_x(i, 1)
+            turn_x(i)
+
+        prepare_x(0)
+        copy_x(0)
+        prepare_x(1)
+        copy_x(1)
+        group_w1(0, 0, nc.scalar.copy)
+        group_w1(1, 0, nc.vector.tensor_copy)
+        quantize_x(0)
+        quantize_w1(1, 0)
+        prepare_x(2)
+        quantize_w1(0, 0)
+        matmul1(0, 0)
+        group_w1(0, 1, nc.scalar.copy)
+        copy_x(2)
+        prepare_x(3)
+        copy_x(3)
+        prepare_b1()
+        group_w1(1, 1, nc.vector.tensor_copy)
+        quantize_w1(0, 1)
+        quantize_w1(1, 1)
+        matmul1(0, 1)
+        matmul1(1, 0)
+        quantize_x(2)
+        scale_x(4, 0)
+        scale_x(4, 1)
+
+        for s in range(TILES):
+            first_plane = 2 * (s - N_LAG)
+            y_on_vector = s >= TILES + Y_SHIFT
+            y_copy = nc.vector.tensor_copy if y_on_vector else nc.scalar.copy
+            first_on_vector = s >= TILES + A_SHIFT
+            tail = s >= TILES + T_SHIFT
+            pool_share = 0 if tail else POOL_SHARE
+            scalar_share = 0 if tail else SCALAR_SHARE
+            on_tile(inverse, s - 2)
+            on_tile(normalize, s - 2, nc.gpsimd if s - 2 < TILES - V_NORM else nc.vector)
+            on_group(group_r, s, N_LAG + 2, 0, nc.gpsimd, 0, pool_share)
+            on_group(group_r, s, N_LAG + 4, 1, nc.gpsimd, 0, pool_share)
+            on_tile(turn_x, s + X_LEAD - 1)
+            on_plane(turn_n, first_plane, first_on_vector)
+            on_tile(add_bias, s)
+            on_tile(variance, s - 1)
+            on_tile(copy_x, s + X_LEAD - 1)
+            on_tile(deviation, s - 1)
+            on_plane(affine_relu, first_plane, first_on_vector)
+            if s > 0 and (A_LATE == 2 or (A_LATE == 1 and s % 2 == 0) or (A_LATE == 3 and s % 2 == 1)):
+                on_tile(matmul1, s + 1, 0)
+            on_tile(matmul1, s + 1, 1)
+            on_group(matmul2, s, N_LAG + 6, 0)
+            on_group(matmul2, s, N_LAG + M2, 1)
+            on_tile(scale_x, s + X_LEAD, 0)
+            on_tile(mean, s)
+            on_tile(scale_x, s + X_LEAD, 1)
+            on_group(add_bias2, s, N_LAG + 6, 0, y_on_vector)
+            on_group(add_bias2, s, N_LAG + M2, 1, y_on_vector)
+            on_plane(turn_n, first_plane + 1, False)
+            on_plane(affine_relu, first_plane + 1, False)
+            on_group(group_r, s, N_LAG + 3, 0, nc.scalar, pool_share, pool_share + scalar_share)
+            on_group(group_r, s, N_LAG + 5, 1, nc.scalar, pool_share, pool_share + scalar_share)
+            on_group(turn_y, s, N_LAG + M2 + 1, 0)
+            on_group(turn_y, s, N_LAG + M2 + 2, 1)
+            on_group(turn_pooled, s, N_LAG + M2 + 3)
+            on_group(store_own, s, N_LAG + M2 + 1, 0, y_copy)
+            on_group(store_own, s, N_LAG + M2 + 2, 1, y_copy)
+            on_group(store_pooled, s, N_LAG + M2 + 3, y_copy)
+            if A_LATE == 0 or (A_LATE == 1 and s % 2 == 0) or (A_LATE == 3 and s % 2 == 1):
+                on_tile(matmul1, s + 2, 0)
+            on_group(pool_nodes, s, N_LAG + M2, 0)
+            on_group(pool_nodes, s, N_LAG + M2 + 1, 1)
+            on_group(group_r, s, N_LAG + 3, 0, nc.vector, pool_share + scalar_share, GROUP)
+            on_group(group_r, s, N_LAG + 5, 1, nc.vector, pool_share + scalar_share, GROUP)
+            on_group(spread_pooled, s, N_LAG + M2 + 2)
+            if s % 2 == 1:
+                on_tile(quantize_x, s + X_LEAD - 2)
+            on_group(quantize_r, s, N_LAG + 3, 0)
+            on_group(quantize_r, s, N_LAG + 5, 1)
+            if s == 0:
+                prepare_columns()
+            if s == 1:
+                group_w2()
+            if s == 3:
+                quantize_w2()
+
+        def plane_pair(k, c):
+            turn_n(k, c, False)
+            turn_n(k, c + 1, True)
+            affine_relu(k, c, False)
+            affine_relu(k, c + 1, True)
+
+        def outputs_first(k):
+            matmul2(k, 0, "hps")
+            matmul2(k, 1, "hps")
+            add_bias2(k, 0, False)
+            add_bias2(k, 1, False)
+
+        def outputs_second(k):
+            turn_y(k, 0, "hps")
+            turn_y(k, 1, "hps")
+            store_own(k, 0, nc.scalar.copy)
+            store_own(k, 1, nc.scalar.copy)
+
+        def outputs_pool(k):
+            pool_nodes(k, 0)
+            pool_nodes(k, 1)
+
+        def outputs_third(k, engine_copy):
+            turn_pooled(k, "ring")
+            store_pooled(k, engine_copy)
+
+        last = TILES - 1
+        k5, k6, k7 = GROUPS - 3, GROUPS - 2, GROUPS - 1
+        inverse(last - 1)
+        normalize(last - 1, nc.gpsimd)
+        variance(last)
+        plane_pair(k6, 4)
+        deviation(last)
+        matmul2(k5, 0, "hps")
+        outputs_third(k5 - 1, nc.scalar.copy)
+        plane_pair(k6, 6)
+        matmul2(k5, 1, "hps")
+        inverse(last)
+        normalize(last, nc.vector)
+        add_bias2(k5, 0, False)
+        add_bias2(k5, 1, False)
+        group_r(k6, 0, nc.vector, 0, GROUP)
+        outputs_second(k5)
+        quantize_r(k6, 0)
+        group_r(k6, 1, nc.vector, 0, GROUP)
+        turn_n(k7, 0, False)
+        affine_relu(k7, 0, False)
+        turn_n(k7, 1, False)
+        affine_relu(k7, 1, False)
+        quantize_r(k6, 1)
+        turn_n(k7, 2, False)
+        affine_relu(k7, 2, False)
+        matmul2(k6, 0, "hps")
+        turn_n(k7, 3, True)
+        affine_relu(k7, 3, True)
+        group_r(k7, 0, nc.gpsimd, 0, TAIL_SHARE)
+        plane_pair(k7, 4)
+        matmul2(k6, 1, "hps")
+        plane_pair(k7, 6)
+        outputs_pool(k5)
+        add_bias2(k6, 0, False)
+        add_bias2(k6, 1, False)
+        group_r(k7, 0, nc.vector, TAIL_SHARE, GROUP)
+        spread_pooled(k5)
+        group_r(k7, 1, nc.vector, 0, GROUP)
+        outputs_second(k6)
+        quantize_r(k7, 0)
+        outputs_third(k5, nc.scalar.copy)
+        quantize_r(k7, 1)
+        outputs_first(k7)
+        outputs_pool(k6)
+        spread_pooled(k6)
+        outputs_third(k6, nc.scalar.copy)
+        outputs_pool(k7)
+        outputs_second(k7)
+        spread_pooled(k7)
+        outputs_third(k7, nc.vector.tensor_copy)

@@ -31,16 +31,23 @@ POLYS = GROUP // L
 ROWS_PER_POLY = P // POLYS
 N_LAG = 6
 X_LEAD = 5
-Y_SHIFT = 20
-A_SHIFT = -4
-T_SHIFT = 20
-V_NORM = 1
-M2 = 7
-TAIL_SHARE = 320
-A_LATE = 1
 H_BANKS = 3
-POOL_SHARE = 256
-SCALAR_SHARE = 0
+POOL_SHARE = 320
+FIRST_POOL_SHARE = 256
+FIRST_SCALAR_SHARE = 64
+W_SHARE = 2
+END_PAIR = 16
+LAST_POOL_SHARE = 256
+V_PLANES = 2
+VT = 2
+B_V = 0
+BIAS_FIRST = 1
+T1 = 512
+G1_AT = 4
+G2_AT = 2
+M_AT = 2
+T2 = 384
+T3 = 128
 
 
 def tile_sub_graph_pa_t_kernel(tc, x_bytes, x_scale, w1, b1, gamma, beta, w2, b2, out):
@@ -108,11 +115,12 @@ def tile_sub_graph_pa_t_kernel(tc, x_bytes, x_scale, w1, b1, gamma, beta, w2, b2
 
         w1_codes, w1_scales, w1_grouped = {}, {}, {}
 
-        def group_w1(g, c, engine_copy):
-            w1_grouped[g, c] = keep.tile([P, PACK, P, PACK], BF16, name="w1grp%d%d" % (g, c), align_bytes=64)
+        def group_w1(g, c, engine_copy, first, last):
+            if (g, c) not in w1_grouped:
+                w1_grouped[g, c] = keep.tile([P, PACK, P, PACK], BF16, name="w1grp%d%d" % (g, c), align_bytes=64)
             engine_copy(
-                out=w1_grouped[g, c][:].rearrange("p t (a i) j -> p a t i j", i=2),
-                in_=w1_raw[g, c][:].rearrange("p j (a i t) -> p a t i j", i=2, t=PACK),
+                out=w1_grouped[g, c][:, first:last, :, :].rearrange("p t (a i) j -> p a t i j", i=2),
+                in_=w1_raw[g, c][:].rearrange("p j (a i t) -> p a t i j", i=2, t=PACK)[:, :, first:last, :, :],
             )
 
         def quantize_w1(g, c):
@@ -269,22 +277,21 @@ def tile_sub_graph_pa_t_kernel(tc, x_bytes, x_scale, w1, b1, gamma, beta, w2, b2
         nt, planes, rg, rq, rs = {}, {}, {}, {}, {}
         y_ps, y, pooled, spread, yt, own, shared = {}, {}, {}, {}, {}, {}, {}
 
-        def turn_n(k, c, on_vector):
-            if on_vector:
-                nt[k, c] = psum.tile([P, TILES_PER_GROUP, P], F32, name="scale%d" % (c // 2 % 2))
-            else:
-                nt[k, c] = psum.tile([P, TILES_PER_GROUP, P], F32, name="ring", bufs=6 - H_BANKS)
-            for j in range(TILES_PER_GROUP):
-                nc.tensor.transpose(nt[k, c][:, j, :], nrm[k * TILES_PER_GROUP + j][:, c * P : (c + 1) * P], ident[:])
+        def turn_n(unit, c, bank, bufs):
+            k, first, count = unit
+            nt[unit, c] = psum.tile([P, count, P], F32, name=bank, bufs=bufs)
+            for j in range(count):
+                rows = nrm[k * TILES_PER_GROUP + first + j]
+                nc.tensor.transpose(nt[unit, c][:, j, :], rows[:, c * P : (c + 1) * P], ident[:])
 
-        def affine_relu(k, c, on_vector):
+        def affine_relu(unit, c, on_vector):
             g, t = divmod(c, PACK)
-            if t == 0:
-                planes[k, g] = work.tile([P, PACK, GROUP], BF16, name="planes", bufs=3)
-            turned = nt[k, c][:].rearrange("p j r -> p (j r)")
+            if (unit, g) not in planes:
+                planes[unit, g] = work.tile([P, PACK, unit[2] * P], BF16, name="planes", bufs=4)
+            turned = nt[unit, c][:].rearrange("p j r -> p (j r)")
             if on_vector:
                 nc.vector.tensor_scalar(
-                    out=planes[k, g][:, t, :],
+                    out=planes[unit, g][:, t, :],
                     in0=turned,
                     scalar1=gamma_col[:, g, t : t + 1],
                     scalar2=beta_col[:, g, t : t + 1],
@@ -293,112 +300,132 @@ def tile_sub_graph_pa_t_kernel(tc, x_bytes, x_scale, w1, b1, gamma, beta, w2, b2
                 )
             else:
                 nc.scalar.activation(
-                    out=planes[k, g][:, t, :],
+                    out=planes[unit, g][:, t, :],
                     in_=turned,
                     func=ACT.Relu,
                     scale=gamma_col[:, g, t : t + 1],
                     bias=beta_col[:, g, t : t + 1],
                 )
 
-        def group_r(k, g, engine, first, last):
+        def group_r(unit, g, engine, first, last):
             if first == last:
                 return
-            if (k, g) not in rg:
-                rg[k, g] = work.tile([P, GROUP, PACK], BF16, name="rg", bufs=2, align_bytes=64)
-            dst = rg[k, g][:, first:last, :].rearrange("p (a i) t -> p a t i", i=4)
-            src = planes[k, g][:, :, first:last].rearrange("p t (a i) -> p a t i", i=4)
+            if (unit, g) not in rg:
+                rg[unit, g] = work.tile([P, unit[2] * P, PACK], BF16, name="rg", bufs=3, align_bytes=64)
+            dst = rg[unit, g][:, first:last, :].rearrange("p (a i) t -> p a t i", i=4)
+            src = planes[unit, g][:, :, first:last].rearrange("p t (a i) -> p a t i", i=4)
             if engine is nc.scalar:
                 nc.scalar.copy(out=dst, in_=src)
             else:
                 engine.tensor_scalar(out=dst, in0=src, scalar1=BF16_MAX, scalar2=0.0, op0=ALU.min, op1=ALU.max)
 
-        def quantize_r(k, g):
-            rq[k, g] = work.tile([P, GROUP], U32, name="rq", bufs=3, align_bytes=64)
-            rs[k, g] = work.tile([P, GROUP], U8, name="rs", bufs=3, align_bytes=64)
+        def quantize_r(unit, g):
+            rq[unit, g] = work.tile([P, unit[2] * P], U32, name="rq", bufs=4, align_bytes=64)
+            rs[unit, g] = work.tile([P, unit[2] * P], U8, name="rs", bufs=4, align_bytes=64)
             nc.vector.quantize_mx(
-                out=rq[k, g][:].bitcast(FP8X4),
-                scales=rs[k, g][:],
-                in_=rg[k, g][:].rearrange("p n t -> p (n t)"),
+                out=rq[unit, g][:].bitcast(FP8X4),
+                scales=rs[unit, g][:],
+                in_=rg[unit, g][:].rearrange("p n t -> p (n t)"),
             )
 
-        def matmul2(k, h, bank="ring"):
-            y_ps[k, h] = psum.tile([P, GROUP], F32, name=bank, bufs=3)
+        def matmul2(unit, h, bank="ring"):
+            y_ps[unit, h] = psum.tile([P, unit[2] * P], F32, name=bank, bufs=3)
             for g in range(PASSES):
                 nc.tensor.matmul_mx(
-                    out=y_ps[k, h][:],
+                    out=y_ps[unit, h][:],
                     lhsT=w2_codes[:, g, h * P : (h + 1) * P].bitcast(FP8X4),
                     lhsT_scale=w2_scales[:, g, h * P : (h + 1) * P],
-                    rhs=rq[k, g][:].bitcast(FP8X4),
-                    rhs_scale=rs[k, g][:],
+                    rhs=rq[unit, g][:].bitcast(FP8X4),
+                    rhs_scale=rs[unit, g][:],
                     start=(g == 0),
                     stop=(g == PASSES - 1),
                 )
 
-        def add_bias2(k, h, on_vector):
-            y[k, h] = work.tile([P, GROUP], F32, name="y", bufs=4)
+        def add_bias2(unit, h, on_vector):
+            y[unit, h] = work.tile([P, unit[2] * P], F32, name="y", bufs=6)
             if on_vector:
                 nc.vector.tensor_scalar(
-                    out=y[k, h][:], in0=y_ps[k, h][:], scalar1=b2_col[:, h : h + 1], scalar2=None, op0=ALU.add
+                    out=y[unit, h][:], in0=y_ps[unit, h][:], scalar1=b2_col[:, h : h + 1], scalar2=None, op0=ALU.add
                 )
             else:
-                nc.scalar.activation(out=y[k, h][:], in_=y_ps[k, h][:], func=ACT.Identity, bias=b2_col[:, h : h + 1])
+                nc.scalar.activation(
+                    out=y[unit, h][:], in_=y_ps[unit, h][:], func=ACT.Identity, bias=b2_col[:, h : h + 1]
+                )
 
-        def pool_nodes(k, h):
+        def pool_nodes(unit, h):
             if h == 0:
-                pooled[k] = work.tile([P, HALVES * POLYS, 1], F32, name="pooled", bufs=2)
+                pooled[unit] = work.tile([P, HALVES * POLYS, 1], F32, name="pooled", bufs=3)
             nc.vector.tensor_reduce(
-                out=pooled[k][:, h * POLYS : (h + 1) * POLYS, 0],
-                in_=y[k, h][:].rearrange("p (j b q) -> p b j q", j=TILES_PER_GROUP, b=POLYS),
+                out=pooled[unit][:, h * POLYS : (h + 1) * POLYS, 0],
+                in_=y[unit, h][:].rearrange("p (j b q) -> p b j q", j=unit[2], b=POLYS),
                 axis=mybir.AxisListType.XY,
                 op=ALU.max,
             )
 
-        def spread_pooled(k):
-            spread[k] = work.tile([P, HALVES * POLYS, ROWS_PER_POLY], F32, name="spread", bufs=2)
-            nc.vector.tensor_copy(
-                out=spread[k][:], in_=pooled[k][:].to_broadcast([P, HALVES * POLYS, ROWS_PER_POLY])
-            )
+        def spread_pooled(unit, other=None):
+            wide = [P, HALVES * POLYS, ROWS_PER_POLY]
+            spread[unit] = work.tile(wide, F32, name="spread", bufs=2)
+            if other is None:
+                nc.vector.tensor_copy(out=spread[unit][:], in_=pooled[unit][:].to_broadcast(wide))
+            else:
+                nc.vector.tensor_tensor(
+                    out=spread[unit][:],
+                    in0=pooled[unit][:].to_broadcast(wide),
+                    in1=pooled[other][:].to_broadcast(wide),
+                    op=ALU.max,
+                )
 
-        def turn_y(k, pair, bank="ring"):
-            yt[k, pair] = psum.tile([P, 2, G], F32, name=bank, bufs=3)
-            for jj in range(2):
-                j = 2 * pair + jj
-                for h in range(HALVES):
-                    nc.tensor.transpose(
-                        yt[k, pair][:, jj, h * P : (h + 1) * P], y[k, h][:, j * P : (j + 1) * P], ident[:]
-                    )
+        def turn_y(unit, h, bank="ring"):
+            yt[unit, h] = psum.tile([P, unit[2], P], F32, name=bank, bufs=3)
+            for j in range(unit[2]):
+                nc.tensor.transpose(yt[unit, h][:, j, :], y[unit, h][:, j * P : (j + 1) * P], ident[:])
 
-        def store_own(k, pair, engine_copy):
-            own[k, pair] = work.tile([P, 2, G], F32, name="own", bufs=4)
-            engine_copy(out=own[k, pair][:], in_=yt[k, pair][:])
-            nc.sync.dma_start(out=out_rows[k, :, 2 * pair : 2 * pair + 2, 0:G], in_=own[k, pair][:])
+        def store_own(unit, h, engine_copy):
+            if h == 0:
+                own[unit] = work.tile([P, TILES_PER_GROUP, G], F32, name="own", bufs=2)
+            engine_copy(out=own[unit][:, :, h * P : (h + 1) * P], in_=yt[unit, h][:])
+            if h == HALVES - 1:
+                nc.sync.dma_start(out=out_rows[unit[0], :, :, 0:G], in_=own[unit][:])
 
-        def turn_pooled(k, bank="ring"):
-            yt[k, 2] = psum.tile([P, 1, G], F32, name=bank, bufs=3)
-            flat = spread[k][:].rearrange("p a q -> p (a q)")
+        def turn_pooled(unit, bank="ring"):
+            yt[unit, 2] = psum.tile([P, 1, G], F32, name=bank, bufs=3)
+            flat = spread[unit][:].rearrange("p a q -> p (a q)")
             for h in range(HALVES):
-                nc.tensor.transpose(yt[k, 2][:, 0, h * P : (h + 1) * P], flat[:, h * P : (h + 1) * P], ident[:])
+                nc.tensor.transpose(yt[unit, 2][:, 0, h * P : (h + 1) * P], flat[:, h * P : (h + 1) * P], ident[:])
 
-        def store_pooled(k, engine_copy):
-            shared[k] = work.tile([P, 1, G], F32, name="shared", bufs=2)
-            engine_copy(out=shared[k][:], in_=yt[k, 2][:])
+        def store_pooled(unit, engine_copy):
+            shared[unit] = work.tile([P, 1, G], F32, name="shared", bufs=3)
+            engine_copy(out=shared[unit][:], in_=yt[unit, 2][:])
             nc.sync.dma_start(
-                out=out_rows[k, :, :, G : 2 * G], in_=shared[k][:].to_broadcast([P, TILES_PER_GROUP, G])
+                out=out_rows[unit[0], :, :, G : 2 * G], in_=shared[unit][:].to_broadcast([P, TILES_PER_GROUP, G])
             )
+
+        def whole(k):
+            return (k, 0, TILES_PER_GROUP)
 
         def on_tile(stage, i, *args):
             if 0 <= i < TILES:
                 stage(i, *args)
 
-        def on_group(stage, s, lag, *args):
-            k, rest = divmod(s - lag, TILES_PER_GROUP)
-            if rest == 0 and 0 <= k < GROUPS:
-                stage(k, *args)
-
-        def on_plane(stage, n, *args):
-            k, c = divmod(n, PASSES * PACK)
+        def on_half(stage, n, *args):
+            k, half = divmod(n, 2)
             if 0 <= k < GROUPS:
-                stage(k, c, *args)
+                stage(whole(k), half, *args)
+
+        def plane(n, t, bank="ring", bufs=3):
+            k, g = divmod(n, 2)
+            if 0 <= k < GROUPS:
+                turn_n(whole(k), PACK * g + t, bank, bufs)
+
+        def relu(n, t, on_vector=False):
+            k, g = divmod(n, 2)
+            if 0 <= k < GROUPS:
+                affine_relu(whole(k), PACK * g + t, on_vector)
+
+        def on_group(stage, n, *args):
+            k, half = divmod(n, 2)
+            if half == 0 and 0 <= k < GROUPS:
+                stage(whole(k), *args)
 
         def prepare_x(i):
             scale_x(i, 0)
@@ -406,161 +433,179 @@ def tile_sub_graph_pa_t_kernel(tc, x_bytes, x_scale, w1, b1, gamma, beta, w2, b2
             turn_x(i)
 
         prepare_x(0)
-        copy_x(0)
+        group_w1(0, 0, nc.scalar.copy, 0, PACK)
         prepare_x(1)
+        copy_x(0)
         copy_x(1)
-        group_w1(0, 0, nc.scalar.copy)
-        group_w1(1, 0, nc.vector.tensor_copy)
-        quantize_x(0)
-        quantize_w1(1, 0)
+        group_w1(1, 0, nc.vector.tensor_copy, 0, PACK)
         prepare_x(2)
         quantize_w1(0, 0)
+        quantize_x(0)
+        quantize_w1(1, 0)
         matmul1(0, 0)
-        group_w1(0, 1, nc.scalar.copy)
-        copy_x(2)
+        group_w1(0, 1, nc.scalar.copy, 0, PACK)
+        group_w1(1, 1, nc.scalar.copy, 0, W_SHARE)
         prepare_x(3)
-        copy_x(3)
-        prepare_b1()
-        group_w1(1, 1, nc.vector.tensor_copy)
+        group_w1(1, 1, nc.vector.tensor_copy, W_SHARE, PACK)
         quantize_w1(0, 1)
+        prepare_b1()
+        copy_x(2)
+        copy_x(3)
         quantize_w1(1, 1)
+        scale_x(4, 0)
+        scale_x(4, 1)
         matmul1(0, 1)
         matmul1(1, 0)
         quantize_x(2)
-        scale_x(4, 0)
-        scale_x(4, 1)
 
-        for s in range(TILES):
-            first_plane = 2 * (s - N_LAG)
-            y_on_vector = s >= TILES + Y_SHIFT
-            y_copy = nc.vector.tensor_copy if y_on_vector else nc.scalar.copy
-            first_on_vector = s >= TILES + A_SHIFT
-            tail = s >= TILES + T_SHIFT
-            pool_share = 0 if tail else POOL_SHARE
-            scalar_share = 0 if tail else SCALAR_SHARE
-            on_tile(inverse, s - 2)
-            on_tile(normalize, s - 2, nc.gpsimd if s - 2 < TILES - V_NORM else nc.vector)
-            on_group(group_r, s, N_LAG + 2, 0, nc.gpsimd, 0, pool_share)
-            on_group(group_r, s, N_LAG + 4, 1, nc.gpsimd, 0, pool_share)
-            on_tile(turn_x, s + X_LEAD - 1)
-            on_plane(turn_n, first_plane, first_on_vector)
-            on_tile(add_bias, s)
-            on_tile(variance, s - 1)
-            on_tile(copy_x, s + X_LEAD - 1)
-            on_tile(deviation, s - 1)
-            on_plane(affine_relu, first_plane, first_on_vector)
-            if s > 0 and (A_LATE == 2 or (A_LATE == 1 and s % 2 == 0) or (A_LATE == 3 and s % 2 == 1)):
-                on_tile(matmul1, s + 1, 0)
-            on_tile(matmul1, s + 1, 1)
-            on_group(matmul2, s, N_LAG + 6, 0)
-            on_group(matmul2, s, N_LAG + M2, 1)
-            on_tile(scale_x, s + X_LEAD, 0)
-            on_tile(mean, s)
-            on_tile(scale_x, s + X_LEAD, 1)
-            on_group(add_bias2, s, N_LAG + 6, 0, y_on_vector)
-            on_group(add_bias2, s, N_LAG + M2, 1, y_on_vector)
-            on_plane(turn_n, first_plane + 1, False)
-            on_plane(affine_relu, first_plane + 1, False)
-            on_group(group_r, s, N_LAG + 3, 0, nc.scalar, pool_share, pool_share + scalar_share)
-            on_group(group_r, s, N_LAG + 5, 1, nc.scalar, pool_share, pool_share + scalar_share)
-            on_group(turn_y, s, N_LAG + M2 + 1, 0)
-            on_group(turn_y, s, N_LAG + M2 + 2, 1)
-            on_group(turn_pooled, s, N_LAG + M2 + 3)
-            on_group(store_own, s, N_LAG + M2 + 1, 0, y_copy)
-            on_group(store_own, s, N_LAG + M2 + 2, 1, y_copy)
-            on_group(store_pooled, s, N_LAG + M2 + 3, y_copy)
-            if A_LATE == 0 or (A_LATE == 1 and s % 2 == 0) or (A_LATE == 3 and s % 2 == 1):
-                on_tile(matmul1, s + 2, 0)
-            on_group(pool_nodes, s, N_LAG + M2, 0)
-            on_group(pool_nodes, s, N_LAG + M2 + 1, 1)
-            on_group(group_r, s, N_LAG + 3, 0, nc.vector, pool_share + scalar_share, GROUP)
-            on_group(group_r, s, N_LAG + 5, 1, nc.vector, pool_share + scalar_share, GROUP)
-            on_group(spread_pooled, s, N_LAG + M2 + 2)
-            if s % 2 == 1:
-                on_tile(quantize_x, s + X_LEAD - 2)
-            on_group(quantize_r, s, N_LAG + 3, 0)
-            on_group(quantize_r, s, N_LAG + 5, 1)
-            if s == 0:
+        for q in range(END_PAIR):
+            even, odd = 2 * q, 2 * q + 1
+            first_group = q < 6
+            pool_share = FIRST_POOL_SHARE if first_group else POOL_SHARE
+            scalar_share = FIRST_SCALAR_SHARE if first_group else 0
+            x_done = even + 4 >= TILES
+            if x_done:
+                pool_share = LAST_POOL_SHARE
+
+            on_tile(inverse, even - 2)
+            on_tile(normalize, even - 2, nc.gpsimd)
+            on_half(group_r, q - 4, nc.gpsimd, 0, pool_share)
+            on_tile(turn_x, even + 4)
+            if x_done and V_PLANES > 0:
+                plane(q - 3, 0, "scale0", 1)
+            else:
+                plane(q - 3, 0)
+            on_tile(add_bias, even)
+            on_tile(variance, even - 1)
+            on_tile(copy_x, even + 4)
+            on_tile(deviation, even - 1)
+            relu(q - 3, 0, x_done and V_PLANES > 0)
+            on_tile(matmul1, odd, 1)
+            on_tile(scale_x, even + 5, 0)
+            on_tile(mean, even)
+            on_tile(scale_x, even + 5, 1)
+            plane(q - 3, 1)
+            relu(q - 3, 1)
+            on_group(turn_pooled, q - 8)
+            on_group(store_pooled, q - 8, nc.scalar.copy)
+            on_tile(matmul1, even + 2, 0)
+            if q == 0:
                 prepare_columns()
-            if s == 1:
+
+            on_half(matmul2, q - 6)
+            on_tile(inverse, odd - 2)
+            on_tile(normalize, odd - 2, nc.gpsimd)
+            on_tile(turn_x, odd + 4)
+            on_tile(add_bias, odd)
+            if BIAS_FIRST:
+                on_half(add_bias2, q - 6, False)
+            on_half(group_r, q - 4, nc.scalar, pool_share, pool_share + scalar_share)
+            on_tile(variance, odd - 1)
+            if not BIAS_FIRST:
+                on_half(add_bias2, q - 6, False)
+            if x_done and V_PLANES > 1:
+                plane(q - 3, 2, "scale1", 1)
+            else:
+                plane(q - 3, 2)
+            on_tile(copy_x, odd + 4)
+            on_tile(deviation, odd - 1)
+            relu(q - 3, 2, x_done and V_PLANES > 1)
+            on_tile(matmul1, even + 2, 1)
+            on_tile(scale_x, odd + 5, 0)
+            on_tile(mean, odd)
+            on_tile(scale_x, odd + 5, 1)
+            plane(q - 3, 3)
+            relu(q - 3, 3)
+            on_half(turn_y, q - 6)
+            on_half(store_own, q - 6, nc.scalar.copy)
+            on_tile(matmul1, odd + 2, 0)
+            on_half(pool_nodes, q - 6)
+            on_half(group_r, q - 4, nc.vector, pool_share + scalar_share, GROUP)
+            on_tile(quantize_x, even + 4)
+            on_group(spread_pooled, q - 7)
+            on_half(quantize_r, q - 4)
+            if q == 0:
                 group_w2()
-            if s == 3:
+            if q == 1:
                 quantize_w2()
 
-        def plane_pair(k, c):
-            turn_n(k, c, False)
-            turn_n(k, c + 1, True)
-            affine_relu(k, c, False)
-            affine_relu(k, c + 1, True)
-
-        def outputs_first(k):
-            matmul2(k, 0, "hps")
-            matmul2(k, 1, "hps")
-            add_bias2(k, 0, False)
-            add_bias2(k, 1, False)
-
-        def outputs_second(k):
-            turn_y(k, 0, "hps")
-            turn_y(k, 1, "hps")
-            store_own(k, 0, nc.scalar.copy)
-            store_own(k, 1, nc.scalar.copy)
-
-        def outputs_pool(k):
-            pool_nodes(k, 0)
-            pool_nodes(k, 1)
-
-        def outputs_third(k, engine_copy):
-            turn_pooled(k, "ring")
-            store_pooled(k, engine_copy)
-
         last = TILES - 1
-        k5, k6, k7 = GROUPS - 3, GROUPS - 2, GROUPS - 1
+        k4, k5, k6, k7 = (whole(k) for k in range(GROUPS - 4, GROUPS))
+
+        def own_store(unit, h, bank):
+            turn_y(unit, h, bank)
+            store_own(unit, h, nc.scalar.copy)
+
+        def pooled_store(unit, bank, engine_copy):
+            turn_pooled(unit, bank)
+            store_pooled(unit, engine_copy)
+
         inverse(last - 1)
         normalize(last - 1, nc.gpsimd)
         variance(last)
-        plane_pair(k6, 4)
+        plane(13, 0, "scale0", 1)
+        plane(13, 2, "scale1", 1)
+        relu(13, 0, True)
         deviation(last)
-        matmul2(k5, 0, "hps")
-        outputs_third(k5 - 1, nc.scalar.copy)
-        plane_pair(k6, 6)
-        matmul2(k5, 1, "hps")
+        pooled_store(k4, "hps", nc.scalar.copy)
+        plane(13, 1)
+        plane(13, 3)
+        relu(13, 2, True)
         inverse(last)
         normalize(last, nc.vector)
+        relu(13, 1)
+        relu(13, 3)
+        matmul2(k5, 0, "hps")
         add_bias2(k5, 0, False)
-        add_bias2(k5, 1, False)
         group_r(k6, 0, nc.vector, 0, GROUP)
-        outputs_second(k5)
+        group_r(k6, 1, nc.gpsimd, 0, T2)
+        pool_nodes(k5, 0)
+        for t in range(PACK):
+            if t % 2 == 1 and VT > t // 2:
+                plane(14, t, "scale%d" % (t // 2), 1)
+                relu(14, t, True)
+            else:
+                plane(14, t)
+                relu(14, t)
+        matmul2(k5, 1, "hps")
+        add_bias2(k5, 1, False)
+        for t in range(PACK):
+            if t % 2 == 1 and VT > 2 + t // 2:
+                plane(15, t, "scale%d" % (t // 2), 1)
+                relu(15, t, True)
+            else:
+                plane(15, t)
+                relu(15, t)
+        pool_nodes(k5, 1)
+        group_r(k6, 1, nc.vector, T2, GROUP)
         quantize_r(k6, 0)
-        group_r(k6, 1, nc.vector, 0, GROUP)
-        turn_n(k7, 0, False)
-        affine_relu(k7, 0, False)
-        turn_n(k7, 1, False)
-        affine_relu(k7, 1, False)
         quantize_r(k6, 1)
-        turn_n(k7, 2, False)
-        affine_relu(k7, 2, False)
-        matmul2(k6, 0, "hps")
-        turn_n(k7, 3, True)
-        affine_relu(k7, 3, True)
-        group_r(k7, 0, nc.gpsimd, 0, TAIL_SHARE)
-        plane_pair(k7, 4)
-        matmul2(k6, 1, "hps")
-        plane_pair(k7, 6)
-        outputs_pool(k5)
-        add_bias2(k6, 0, False)
-        add_bias2(k6, 1, False)
-        group_r(k7, 0, nc.vector, TAIL_SHARE, GROUP)
         spread_pooled(k5)
-        group_r(k7, 1, nc.vector, 0, GROUP)
-        outputs_second(k6)
+        group_r(k7, 0, nc.vector, 0, GROUP)
+        own_store(k5, 0, "ring")
+        own_store(k5, 1, "ring")
+        matmul2(k6, 0, "hps")
+        add_bias2(k6, 0, False)
+        pooled_store(k5, "ring", nc.scalar.copy)
+        matmul2(k6, 1, "hps")
+        group_r(k7, 1, nc.scalar, 0, T3)
+        add_bias2(k6, 1, False)
         quantize_r(k7, 0)
-        outputs_third(k5, nc.scalar.copy)
+        group_r(k7, 1, nc.vector, T3, GROUP)
+        pool_nodes(k6, 0)
         quantize_r(k7, 1)
-        outputs_first(k7)
-        outputs_pool(k6)
+        own_store(k6, 0, "ring")
+        own_store(k6, 1, "ring")
+        pool_nodes(k6, 1)
+        matmul2(k7, 0, "hps")
+        matmul2(k7, 1, "hps")
+        add_bias2(k7, 0, False)
+        add_bias2(k7, 1, B_V)
         spread_pooled(k6)
-        outputs_third(k6, nc.scalar.copy)
-        outputs_pool(k7)
-        outputs_second(k7)
+        pooled_store(k6, "ring", nc.vector.tensor_copy)
+        pool_nodes(k7, 0)
+        pool_nodes(k7, 1)
+        own_store(k7, 0, "ring")
         spread_pooled(k7)
-        outputs_third(k7, nc.vector.tensor_copy)
+        own_store(k7, 1, "ring")
+        pooled_store(k7, "hps", nc.vector.tensor_copy)

@@ -34,20 +34,25 @@ X_LEAD = 5
 H_BANKS = 3
 POOL_SHARE = 320
 FIRST_POOL_SHARE = 256
-FIRST_SCALAR_SHARE = 64
+FIRST_SCALAR_SHARE = 128
 W_SHARE = 2
-END_PAIR = 16
+PAIRS = 16
+W2_A = 0
+W2_B = 2
+END_SHARE = 192
+POOLED_V = 0
+INV_EARLY = 0
 LAST_POOL_SHARE = 256
 V_PLANES = 2
-VT = 2
+VT = 1
 B_V = 0
 BIAS_FIRST = 1
 T1 = 512
 G1_AT = 4
 G2_AT = 2
 M_AT = 2
-T2 = 384
-T3 = 128
+T2 = 320
+T3 = 192
 
 
 def tile_sub_graph_pa_t_kernel(tc, x_bytes, x_scale, w1, b1, gamma, beta, w2, b2, out):
@@ -148,12 +153,11 @@ def tile_sub_graph_pa_t_kernel(tc, x_bytes, x_scale, w1, b1, gamma, beta, w2, b2
             nc.scalar.copy(out=beta_col[:], in_=beta_raw[:])
             nc.scalar.copy(out=b2_col[:], in_=b2_raw[:, :, 0])
 
-        def group_w2():
-            for g in range(PASSES):
-                nc.scalar.copy(
-                    out=w2_grouped[:, g, :, :].rearrange("p (a i) j -> p a j i", i=4),
-                    in_=w2_raw[:, g, :, :].rearrange("p j (a i) -> p a j i", i=4),
-                )
+        def group_w2(g):
+            nc.scalar.copy(
+                out=w2_grouped[:, g, :, :].rearrange("p (a i) j -> p a j i", i=4),
+                in_=w2_raw[:, g, :, :].rearrange("p j (a i) -> p a j i", i=4),
+            )
 
         def quantize_w2():
             nc.vector.quantize_mx(
@@ -458,28 +462,24 @@ def tile_sub_graph_pa_t_kernel(tc, x_bytes, x_scale, w1, b1, gamma, beta, w2, b2
         matmul1(1, 0)
         quantize_x(2)
 
-        for q in range(END_PAIR):
+        for q in range(PAIRS - 2):
             even, odd = 2 * q, 2 * q + 1
-            first_group = q < 6
-            pool_share = FIRST_POOL_SHARE if first_group else POOL_SHARE
-            scalar_share = FIRST_SCALAR_SHARE if first_group else 0
-            x_done = even + 4 >= TILES
-            if x_done:
+            pool_share, scalar_share = POOL_SHARE, 0
+            if q < 6:
+                pool_share, scalar_share = FIRST_POOL_SHARE, FIRST_SCALAR_SHARE
+            if odd + 5 >= TILES:
                 pool_share = LAST_POOL_SHARE
 
             on_tile(inverse, even - 2)
             on_tile(normalize, even - 2, nc.gpsimd)
             on_half(group_r, q - 4, nc.gpsimd, 0, pool_share)
             on_tile(turn_x, even + 4)
-            if x_done and V_PLANES > 0:
-                plane(q - 3, 0, "scale0", 1)
-            else:
-                plane(q - 3, 0)
+            plane(q - 3, 0)
             on_tile(add_bias, even)
             on_tile(variance, even - 1)
             on_tile(copy_x, even + 4)
             on_tile(deviation, even - 1)
-            relu(q - 3, 0, x_done and V_PLANES > 0)
+            relu(q - 3, 0)
             on_tile(matmul1, odd, 1)
             on_tile(scale_x, even + 5, 0)
             on_tile(mean, even)
@@ -491,25 +491,23 @@ def tile_sub_graph_pa_t_kernel(tc, x_bytes, x_scale, w1, b1, gamma, beta, w2, b2
             on_tile(matmul1, even + 2, 0)
             if q == 0:
                 prepare_columns()
+            if q == W2_A:
+                group_w2(0)
+            if q == W2_B:
+                group_w2(1)
 
             on_half(matmul2, q - 6)
             on_tile(inverse, odd - 2)
             on_tile(normalize, odd - 2, nc.gpsimd)
             on_tile(turn_x, odd + 4)
             on_tile(add_bias, odd)
-            if BIAS_FIRST:
-                on_half(add_bias2, q - 6, False)
-            on_half(group_r, q - 4, nc.scalar, pool_share, pool_share + scalar_share)
+            on_half(add_bias2, q - 6, False)
             on_tile(variance, odd - 1)
-            if not BIAS_FIRST:
-                on_half(add_bias2, q - 6, False)
-            if x_done and V_PLANES > 1:
-                plane(q - 3, 2, "scale1", 1)
-            else:
-                plane(q - 3, 2)
+            plane(q - 3, 2)
             on_tile(copy_x, odd + 4)
             on_tile(deviation, odd - 1)
-            relu(q - 3, 2, x_done and V_PLANES > 1)
+            on_half(group_r, q - 4, nc.scalar, pool_share, pool_share + scalar_share)
+            relu(q - 3, 2)
             on_tile(matmul1, even + 2, 1)
             on_tile(scale_x, odd + 5, 0)
             on_tile(mean, odd)
@@ -524,10 +522,46 @@ def tile_sub_graph_pa_t_kernel(tc, x_bytes, x_scale, w1, b1, gamma, beta, w2, b2
             on_tile(quantize_x, even + 4)
             on_group(spread_pooled, q - 7)
             on_half(quantize_r, q - 4)
-            if q == 0:
-                group_w2()
-            if q == 1:
+            if q == W2_B + 1:
                 quantize_w2()
+
+        for q in range(PAIRS - 2, PAIRS):
+            even, odd = 2 * q, 2 * q + 1
+            inverse(even - 2)
+            normalize(even - 2, nc.gpsimd)
+            on_half(group_r, q - 4, nc.gpsimd, 0, END_SHARE)
+            plane(q - 3, 0, "scale0", 1)
+            on_half(matmul2, q - 6)
+            add_bias(even)
+            variance(even - 1)
+            on_half(add_bias2, q - 6, False)
+            deviation(even - 1)
+            matmul1(odd, 1)
+            plane(q - 3, 1)
+            plane(q - 3, 2, "scale1", 1)
+            relu(q - 3, 0, True)
+            mean(even)
+            relu(q - 3, 1)
+            variance(even)
+            on_tile(matmul1, even + 2, 0)
+            inverse(odd - 2)
+            normalize(odd - 2, nc.gpsimd)
+            add_bias(odd)
+            plane(q - 3, 3)
+            relu(q - 3, 3)
+            deviation(even)
+            on_half(turn_y, q - 6)
+            on_half(store_own, q - 6, nc.scalar.copy)
+            on_group(turn_pooled, q - 8)
+            on_group(store_pooled, q - 8, nc.scalar.copy)
+            on_tile(matmul1, even + 2, 1)
+            on_tile(matmul1, odd + 2, 0)
+            relu(q - 3, 2, True)
+            mean(odd)
+            on_half(pool_nodes, q - 6)
+            on_half(group_r, q - 4, nc.vector, END_SHARE, GROUP)
+            on_group(spread_pooled, q - 7)
+            on_half(quantize_r, q - 4)
 
         last = TILES - 1
         k4, k5, k6, k7 = (whole(k) for k in range(GROUPS - 4, GROUPS))
@@ -540,29 +574,29 @@ def tile_sub_graph_pa_t_kernel(tc, x_bytes, x_scale, w1, b1, gamma, beta, w2, b2
             turn_pooled(unit, bank)
             store_pooled(unit, engine_copy)
 
-        inverse(last - 1)
-        normalize(last - 1, nc.gpsimd)
         variance(last)
-        plane(13, 0, "scale0", 1)
-        plane(13, 2, "scale1", 1)
-        relu(13, 0, True)
-        deviation(last)
-        pooled_store(k4, "hps", nc.scalar.copy)
+        plane(13, 0)
         plane(13, 1)
-        plane(13, 3)
-        relu(13, 2, True)
+        relu(13, 0)
+        deviation(last)
+        inverse(last - 1)
+        normalize(last - 1, nc.vector)
         inverse(last)
         normalize(last, nc.vector)
+        plane(13, 2)
+        plane(13, 3, "scale0", 1)
         relu(13, 1)
-        relu(13, 3)
+        pooled_store(k4, "hps", nc.scalar.copy)
+        relu(13, 2)
         matmul2(k5, 0, "hps")
         add_bias2(k5, 0, False)
         group_r(k6, 0, nc.vector, 0, GROUP)
+        relu(13, 3, True)
         group_r(k6, 1, nc.gpsimd, 0, T2)
         pool_nodes(k5, 0)
         for t in range(PACK):
             if t % 2 == 1 and VT > t // 2:
-                plane(14, t, "scale%d" % (t // 2), 1)
+                plane(14, t, "scale%d" % (1 - t // 2), 1)
                 relu(14, t, True)
             else:
                 plane(14, t)
@@ -580,31 +614,31 @@ def tile_sub_graph_pa_t_kernel(tc, x_bytes, x_scale, w1, b1, gamma, beta, w2, b2
         group_r(k6, 1, nc.vector, T2, GROUP)
         quantize_r(k6, 0)
         quantize_r(k6, 1)
-        spread_pooled(k5)
         group_r(k7, 0, nc.vector, 0, GROUP)
         own_store(k5, 0, "ring")
         own_store(k5, 1, "ring")
         matmul2(k6, 0, "hps")
-        add_bias2(k6, 0, False)
-        pooled_store(k5, "ring", nc.scalar.copy)
-        matmul2(k6, 1, "hps")
         group_r(k7, 1, nc.scalar, 0, T3)
+        add_bias2(k6, 0, False)
+        matmul2(k6, 1, "hps")
         add_bias2(k6, 1, False)
+        spread_pooled(k5)
         quantize_r(k7, 0)
         group_r(k7, 1, nc.vector, T3, GROUP)
-        pool_nodes(k6, 0)
+        pooled_store(k5, "ring", nc.scalar.copy)
         quantize_r(k7, 1)
         own_store(k6, 0, "ring")
         own_store(k6, 1, "ring")
+        pool_nodes(k6, 0)
         pool_nodes(k6, 1)
         matmul2(k7, 0, "hps")
         matmul2(k7, 1, "hps")
         add_bias2(k7, 0, False)
-        add_bias2(k7, 1, B_V)
+        add_bias2(k7, 1, False)
         spread_pooled(k6)
-        pooled_store(k6, "ring", nc.vector.tensor_copy)
         pool_nodes(k7, 0)
         pool_nodes(k7, 1)
+        pooled_store(k6, "ring", nc.scalar.copy)
         own_store(k7, 0, "ring")
         spread_pooled(k7)
         own_store(k7, 1, "ring")

@@ -5,7 +5,6 @@ from concourse.masks import make_identity
 
 B, L, H, G = 64, 64, 1024, 256
 EPS = 1e-5
-BF16_MAX = 3.3895313892515355e38
 FLOPS = 2 * B * L * H * (H + G)
 
 F32 = mybir.dt.float32
@@ -26,39 +25,33 @@ TILES_PER_GROUP = 4
 GROUP = P * TILES_PER_GROUP
 GROUPS = B * L // GROUP
 TILES = GROUPS * TILES_PER_GROUP
+PAIRS = TILES // 2
 HALVES = G // P
 POLYS = GROUP // L
 ROWS_PER_POLY = P // POLYS
-N_LAG = 6
-X_LEAD = 5
+BF16_MAX = 3.3895313892515355e38
+
 H_BANKS = 3
+RING_BANKS = 3
+
+PLANE_LAG = 3
+QUANT_LAG = 4
+OUT_LAG = 6
+SPREAD_LAG = 7
+POOLED_LAG = 8
+SCALE_LEAD = 5
+TURN_LEAD = 4
+
 POOL_SHARE = 320
-FIRST_POOL_SHARE = 256
-FIRST_SCALAR_SHARE = 128
-W_SHARE = 2
-PAIRS = 16
-W2_A = 0
-W2_B = 2
-END_SHARE = 192
-POOLED_V = 0
-INV_EARLY = 0
-LAST_POOL_SHARE = 256
-V_PLANES = 2
-VT = 1
-B_V = 0
-BIAS_FIRST = 1
-T1 = 512
-G1_AT = 4
-G2_AT = 2
-M_AT = 2
-T2 = 320
-T3 = 192
+POOL_SHARE_LONG = 384
+POOL_SHARE_SHORT = 192
+SCALAR_SHARE = 128
 
 
 def tile_sub_graph_pa_t_kernel(tc, x_bytes, x_scale, w1, b1, gamma, beta, w2, b2, out):
     nc = tc.nc
-    x_rows = x_bytes.rearrange("b l h -> (b l) h").rearrange("(k p j) h -> k p j h", p=P, j=TILES_PER_GROUP)
-    out_rows = out.rearrange("b l c -> (b l) c").rearrange("(k p j) c -> k p j c", p=P, j=TILES_PER_GROUP)
+    x_rows = x_bytes.rearrange("b l h -> (b l) h").rearrange("(n p j) h -> n p j h", p=P, j=TILES_PER_GROUP)
+    out_rows = out.rearrange("b l c -> (b l) c").rearrange("(n p j) c -> n p j c", p=P, j=TILES_PER_GROUP)
 
     with ExitStack() as ctx:
         keep = ctx.enter_context(tc.tile_pool(name="keep", bufs=1))
@@ -66,19 +59,25 @@ def tile_sub_graph_pa_t_kernel(tc, x_bytes, x_scale, w1, b1, gamma, beta, w2, b2
         psum = ctx.enter_context(tc.psum_pool(name="psum", bufs=1))
         ctx.enter_context(tc.manual_schedule())
 
+        bank_bufs = {"scale0": 1, "scale1": 1, "h": H_BANKS, "ring": RING_BANKS}
+
+        def psum_tile(shape, bank):
+            return psum.tile(shape, F32, name=bank, bufs=bank_bufs[bank])
+
         ident = keep.tile([P, P], F32)
         make_identity(nc, ident[:])
 
         scale_col = keep.tile([P, PASSES, PACK], F32)
         nc.sync.dma_start(out=scale_col[:], in_=x_scale.rearrange("a b (g p t) -> p (a b g) t", p=P, t=PACK))
+
         xb = {}
 
         def load_x(first, count):
-            k, j = divmod(first, TILES_PER_GROUP)
+            n, j = divmod(first, TILES_PER_GROUP)
             rows = keep.tile([P, count, H], U8, name="xbytes%d" % first)
-            nc.sync.dma_start(out=rows[:], in_=x_rows[k, :, j : j + count, :])
-            for n in range(count):
-                xb[first + n] = rows[:, n, :]
+            nc.sync.dma_start(out=rows[:], in_=x_rows[n, :, j : j + count, :])
+            for step in range(count):
+                xb[first + step] = rows[:, step, :]
 
         w1_raw = {}
 
@@ -95,7 +94,7 @@ def tile_sub_graph_pa_t_kernel(tc, x_bytes, x_scale, w1, b1, gamma, beta, w2, b2
         load_w1(1, 1)
         b1_raw = keep.tile([P, H], BF16)
         nc.sync.dma_start(out=b1_raw[:], in_=b1.partition_broadcast(P))
-        load_x(4, 4)
+        load_x(TILES_PER_GROUP, TILES_PER_GROUP)
         gamma_raw = keep.tile([P, PASSES, PACK], BF16)
         nc.sync.dma_start(out=gamma_raw[:], in_=gamma.rearrange("(g p t) -> p g t", p=P, t=PACK))
         beta_raw = keep.tile([P, PASSES, PACK], BF16)
@@ -108,17 +107,17 @@ def tile_sub_graph_pa_t_kernel(tc, x_bytes, x_scale, w1, b1, gamma, beta, w2, b2
         b2_raw = keep.tile([P, HALVES, 2], BF16)
         with nc.allow_non_contiguous_dma(reason="one bias value to a partition and half"):
             nc.sync.dma_start(out=b2_raw[:, :, 0], in_=b2.rearrange("(h p) -> p h", p=P))
-        for k in range(2, GROUPS):
-            load_x(k * TILES_PER_GROUP, TILES_PER_GROUP)
+        for n in range(2, GROUPS):
+            load_x(n * TILES_PER_GROUP, TILES_PER_GROUP)
 
         scale_row = []
         for g in range(PASSES):
-            bank = psum.tile([P, P, PACK], F32, name="scale%d" % g)
+            bank = psum_tile([P, P, PACK], "scale%d" % g)
             for t in range(PACK):
                 nc.tensor.transpose(bank[:, :, t], scale_col[:, g, t : t + 1].to_broadcast([P, P]), ident[:])
             scale_row.append(bank)
 
-        w1_codes, w1_scales, w1_grouped = {}, {}, {}
+        w1_grouped, w1_codes, w1_scales = {}, {}, {}
 
         def group_w1(g, c, engine_copy, first, last):
             if (g, c) not in w1_grouped:
@@ -166,81 +165,80 @@ def tile_sub_graph_pa_t_kernel(tc, x_bytes, x_scale, w1, b1, gamma, beta, w2, b2
                 in_=w2_grouped[:].rearrange("p g n j -> p (g n j)"),
             )
 
-        xw, xt, xg, xq, xs = {}, {}, {}, {}, {}
-        h_ps, hb, sums, negmu, ssq, std, rstd, nrm = {}, {}, {}, {}, {}, {}, {}, {}
+        x_wide, x_turned, x_grouped, x_codes, x_scales = {}, {}, {}, {}, {}
+        h_ps, hb, sums, neg_mean, sum_sq, std, rstd, normed = {}, {}, {}, {}, {}, {}, {}, {}
 
         def scale_x(i, g):
-            k, j = divmod(i, TILES_PER_GROUP)
             if g == 0:
-                xw[i] = work.tile([P, H], BF16, name="xw", bufs=3)
+                x_wide[i] = work.tile([P, H], BF16, name="x_wide", bufs=3)
             cols = slice(g * K_PASS, (g + 1) * K_PASS)
             nc.vector.tensor_tensor(
-                out=xw[i][:, cols],
+                out=x_wide[i][:, cols],
                 in0=xb[i][:, cols].bitcast(FP8),
                 in1=scale_row[g][:].rearrange("p m t -> p (m t)"),
                 op=ALU.mult,
             )
 
         def turn_x(i):
-            xt[i] = psum.tile([P, PASSES, 2, P], F32, name="ring", bufs=6 - H_BANKS)
-            words = xw[i][:].bitcast(F32)
+            x_turned[i] = psum_tile([P, PASSES, 2, P], "ring")
+            words = x_wide[i][:].bitcast(F32)
             for g in range(PASSES):
                 for u in range(2):
-                    nc.tensor.transpose(xt[i][:, g, u, :], words[:, 2 * P * g + u : 2 * P * (g + 1) : 2], ident[:])
+                    every_second = words[:, 2 * P * g + u : 2 * P * (g + 1) : 2]
+                    nc.tensor.transpose(x_turned[i][:, g, u, :], every_second, ident[:])
 
-        def copy_x(i):
-            pair, n = divmod(i, 2)
-            if n == 0:
-                xg[pair] = work.tile([P, 2, H], BF16, name="xg", bufs=2, align_bytes=64)
-            nc.scalar.copy(
-                out=xg[pair][:, n, :].bitcast(F32).rearrange("p (g r u) -> p g r u", g=PASSES, u=2),
-                in_=xt[i][:].rearrange("p g u r -> p g r u"),
+        def copy_x(i, engine_copy):
+            pair, place = divmod(i, 2)
+            if place == 0:
+                x_grouped[pair] = work.tile([P, 2, H], BF16, name="x_grouped", bufs=2, align_bytes=64)
+            engine_copy(
+                out=x_grouped[pair][:, place, :].bitcast(F32).rearrange("p (g r u) -> p g r u", g=PASSES, u=2),
+                in_=x_turned[i][:].rearrange("p g u r -> p g r u"),
             )
 
         def quantize_x(i):
-            pair = i // 2
-            codes = work.tile([P, 2, PASSES, P], U32, name="xq", bufs=3, align_bytes=64)
-            scales = work.tile([P, 2, PASSES, P], U8, name="xs", bufs=3, align_bytes=64)
+            codes = work.tile([P, 2, PASSES, P], U32, name="x_codes", bufs=3, align_bytes=64)
+            scales = work.tile([P, 2, PASSES, P], U8, name="x_scales", bufs=3, align_bytes=64)
             nc.vector.quantize_mx(
                 out=codes[:].rearrange("p n g r -> p (n g r)").bitcast(FP8X4),
                 scales=scales[:].rearrange("p n g r -> p (n g r)"),
-                in_=xg[pair][:].rearrange("p n c -> p (n c)"),
+                in_=x_grouped[i // 2][:].rearrange("p n c -> p (n c)"),
             )
-            for n in range(2):
-                xq[2 * pair + n] = codes[:, n, :, :]
-                xs[2 * pair + n] = scales[:, n, :, :]
+            for place in range(2):
+                x_codes[i + place] = codes[:, place, :, :]
+                x_scales[i + place] = scales[:, place, :, :]
 
         def matmul1(i, c):
-            h_ps[i, c] = psum.tile([P, BANK], F32, name="hps", bufs=H_BANKS)
+            h_ps[i, c] = psum_tile([P, BANK], "h")
             for g in range(PASSES):
                 nc.tensor.matmul_mx(
                     out=h_ps[i, c][:],
-                    lhsT=xq[i][:, g, :].bitcast(FP8X4),
-                    lhsT_scale=xs[i][:, g, :],
+                    lhsT=x_codes[i][:, g, :].bitcast(FP8X4),
+                    lhsT_scale=x_scales[i][:, g, :],
                     rhs=w1_codes[g, c][:].bitcast(FP8X4),
                     rhs_scale=w1_scales[g, c][:],
                     start=(g == 0),
                     stop=(g == PASSES - 1),
                 )
 
-        def add_bias(i):
-            hb[i] = work.tile([P, PASSES, BANK], F32, name="hb", bufs=4)
-            sums[i] = work.tile([P, PASSES], F32, name="sums", bufs=3)
-            for c in range(PASSES):
-                nc.vector.scalar_tensor_tensor(
-                    out=hb[i][:, c, :],
-                    in0=h_ps[i, c][:],
-                    scalar=1.0,
-                    in1=b1_row[:, c, :, :].rearrange("p t m -> p (t m)"),
-                    op0=ALU.mult,
-                    op1=ALU.add,
-                    accum_out=sums[i][:, c : c + 1],
-                )
+        def add_b1(i, c):
+            if c == 0:
+                hb[i] = work.tile([P, PASSES, BANK], F32, name="hb", bufs=4)
+                sums[i] = work.tile([P, PASSES], F32, name="sums", bufs=3)
+            nc.vector.scalar_tensor_tensor(
+                out=hb[i][:, c, :],
+                in0=h_ps[i, c][:],
+                scalar=1.0,
+                in1=b1_row[:, c, :, :].rearrange("p t m -> p (t m)"),
+                op0=ALU.mult,
+                op1=ALU.add,
+                accum_out=sums[i][:, c : c + 1],
+            )
 
         def mean(i):
-            negmu[i] = work.tile([P, 1], F32, name="negmu", bufs=4)
+            neg_mean[i] = work.tile([P, 1], F32, name="neg_mean", bufs=4)
             nc.vector.tensor_scalar(
-                out=negmu[i][:],
+                out=neg_mean[i][:],
                 in0=sums[i][:, 0:1],
                 scalar1=sums[i][:, 1:2],
                 scalar2=-1.0 / H,
@@ -250,211 +248,197 @@ def tile_sub_graph_pa_t_kernel(tc, x_bytes, x_scale, w1, b1, gamma, beta, w2, b2
 
         def variance(i):
             squares = work.tile([P, H], BF16, name="squares", bufs=2)
-            ssq[i] = work.tile([P, 1], F32, name="ssq", bufs=3)
+            sum_sq[i] = work.tile([P, 1], F32, name="sum_sq", bufs=3)
             nc.scalar.activation(
                 out=squares[:],
                 in_=hb[i][:].rearrange("p c n -> p (c n)"),
                 func=ACT.Square,
-                bias=negmu[i][:],
-                accum_out=ssq[i][:],
+                bias=neg_mean[i][:],
+                accum_out=sum_sq[i][:],
             )
 
         def deviation(i):
             std[i] = work.tile([P, 1], F32, name="std", bufs=3)
-            nc.scalar.activation(out=std[i][:], in_=ssq[i][:], func=ACT.Sqrt, scale=1.0 / H, bias=EPS)
-
-        def inverse(i):
-            rstd[i] = work.tile([P, 1], F32, name="rstd", bufs=3)
-            nc.vector.reciprocal(out=rstd[i][:], in_=std[i][:])
+            nc.scalar.activation(out=std[i][:], in_=sum_sq[i][:], func=ACT.Sqrt, scale=1.0 / H, bias=EPS)
 
         def normalize(i, engine):
-            nrm[i] = work.tile([P, H], F32, name="nrm", bufs=8)
+            rstd[i] = work.tile([P, 1], F32, name="rstd", bufs=3)
+            nc.vector.reciprocal(out=rstd[i][:], in_=std[i][:])
+            normed[i] = work.tile([P, H], F32, name="normed", bufs=8)
             engine.tensor_scalar(
-                out=nrm[i][:],
+                out=normed[i][:],
                 in0=hb[i][:].rearrange("p c n -> p (c n)"),
-                scalar1=negmu[i][:],
+                scalar1=neg_mean[i][:],
                 scalar2=rstd[i][:],
                 op0=ALU.add,
                 op1=ALU.mult,
             )
 
-        nt, planes, rg, rq, rs = {}, {}, {}, {}, {}
-        y_ps, y, pooled, spread, yt, own, shared = {}, {}, {}, {}, {}, {}, {}
+        n_turned, planes, r_grouped, r_codes, r_scales = {}, {}, {}, {}, {}
+        y_ps, y, pooled, spread, own_ps, own, pooled_ps = {}, {}, {}, {}, {}, {}, {}
 
-        def turn_n(unit, c, bank, bufs):
-            k, first, count = unit
-            nt[unit, c] = psum.tile([P, count, P], F32, name=bank, bufs=bufs)
-            for j in range(count):
-                rows = nrm[k * TILES_PER_GROUP + first + j]
-                nc.tensor.transpose(nt[unit, c][:, j, :], rows[:, c * P : (c + 1) * P], ident[:])
+        def turn_plane(m, t, bank):
+            n, g = divmod(m, 2)
+            first = g * BANK + t * P
+            n_turned[m, t] = psum_tile([P, TILES_PER_GROUP, P], bank)
+            for j in range(TILES_PER_GROUP):
+                rows = normed[n * TILES_PER_GROUP + j]
+                nc.tensor.transpose(n_turned[m, t][:, j, :], rows[:, first : first + P], ident[:])
 
-        def affine_relu(unit, c, on_vector):
-            g, t = divmod(c, PACK)
-            if (unit, g) not in planes:
-                planes[unit, g] = work.tile([P, PACK, unit[2] * P], BF16, name="planes", bufs=4)
-            turned = nt[unit, c][:].rearrange("p j r -> p (j r)")
-            if on_vector:
-                nc.vector.tensor_scalar(
-                    out=planes[unit, g][:, t, :],
-                    in0=turned,
-                    scalar1=gamma_col[:, g, t : t + 1],
-                    scalar2=beta_col[:, g, t : t + 1],
-                    op0=ALU.mult,
-                    op1=ALU.add,
-                )
-            else:
-                nc.scalar.activation(
-                    out=planes[unit, g][:, t, :],
-                    in_=turned,
-                    func=ACT.Relu,
-                    scale=gamma_col[:, g, t : t + 1],
-                    bias=beta_col[:, g, t : t + 1],
-                )
+        def plane_out(m, t):
+            if m not in planes:
+                planes[m] = work.tile([P, PACK, GROUP], BF16, name="planes", bufs=4)
+            return planes[m][:, t, :]
 
-        def group_r(unit, g, engine, first, last):
-            if first == last:
-                return
-            if (unit, g) not in rg:
-                rg[unit, g] = work.tile([P, unit[2] * P, PACK], BF16, name="rg", bufs=3, align_bytes=64)
-            dst = rg[unit, g][:, first:last, :].rearrange("p (a i) t -> p a t i", i=4)
-            src = planes[unit, g][:, :, first:last].rearrange("p t (a i) -> p a t i", i=4)
-            if engine is nc.scalar:
-                nc.scalar.copy(out=dst, in_=src)
-            else:
-                engine.tensor_scalar(out=dst, in0=src, scalar1=BF16_MAX, scalar2=0.0, op0=ALU.min, op1=ALU.max)
-
-        def quantize_r(unit, g):
-            rq[unit, g] = work.tile([P, unit[2] * P], U32, name="rq", bufs=4, align_bytes=64)
-            rs[unit, g] = work.tile([P, unit[2] * P], U8, name="rs", bufs=4, align_bytes=64)
-            nc.vector.quantize_mx(
-                out=rq[unit, g][:].bitcast(FP8X4),
-                scales=rs[unit, g][:],
-                in_=rg[unit, g][:].rearrange("p n t -> p (n t)"),
+        def relu_plane(m, t):
+            nc.scalar.activation(
+                out=plane_out(m, t),
+                in_=n_turned[m, t][:].rearrange("p j r -> p (j r)"),
+                func=ACT.Relu,
+                scale=gamma_col[:, m % 2, t : t + 1],
+                bias=beta_col[:, m % 2, t : t + 1],
             )
 
-        def matmul2(unit, h, bank="ring"):
-            y_ps[unit, h] = psum.tile([P, unit[2] * P], F32, name=bank, bufs=3)
+        def affine_plane(m, t):
+            nc.vector.tensor_scalar(
+                out=plane_out(m, t),
+                in0=n_turned[m, t][:].rearrange("p j r -> p (j r)"),
+                scalar1=gamma_col[:, m % 2, t : t + 1],
+                scalar2=beta_col[:, m % 2, t : t + 1],
+                op0=ALU.mult,
+                op1=ALU.add,
+            )
+
+        def group_out(m):
+            if m not in r_grouped:
+                r_grouped[m] = work.tile([P, GROUP, PACK], BF16, name="r_grouped", bufs=3, align_bytes=64)
+            return r_grouped[m]
+
+        def group_r_gpsimd(m, first, last):
+            nc.gpsimd.tensor_scalar(
+                out=group_out(m)[:, first:last, :],
+                in0=planes[m][:, :, first:last].rearrange("p t n -> p n t"),
+                scalar1=BF16_MAX,
+                scalar2=0.0,
+                op0=ALU.min,
+                op1=ALU.max,
+            )
+
+        def group_r_vector(m, first, last):
+            nc.vector.tensor_scalar(
+                out=group_out(m)[:, first:last, :].rearrange("p (a i) t -> p a t i", i=4),
+                in0=planes[m][:, :, first:last].rearrange("p t (a i) -> p a t i", i=4),
+                scalar1=BF16_MAX,
+                scalar2=0.0,
+                op0=ALU.min,
+                op1=ALU.max,
+            )
+
+        def group_r_scalar(m, first, last):
+            nc.scalar.copy(
+                out=group_out(m)[:, first:last, :].rearrange("p (a i) t -> p a t i", i=4),
+                in_=planes[m][:, :, first:last].rearrange("p t (a i) -> p a t i", i=4),
+            )
+
+        def quantize_r(m):
+            r_codes[m] = work.tile([P, GROUP], U32, name="r_codes", bufs=4, align_bytes=64)
+            r_scales[m] = work.tile([P, GROUP], U8, name="r_scales", bufs=4, align_bytes=64)
+            nc.vector.quantize_mx(
+                out=r_codes[m][:].bitcast(FP8X4),
+                scales=r_scales[m][:],
+                in_=r_grouped[m][:].rearrange("p n t -> p (n t)"),
+            )
+
+        def matmul2(m, bank):
+            n, h = divmod(m, 2)
+            y_ps[m] = psum_tile([P, GROUP], bank)
             for g in range(PASSES):
                 nc.tensor.matmul_mx(
-                    out=y_ps[unit, h][:],
+                    out=y_ps[m][:],
                     lhsT=w2_codes[:, g, h * P : (h + 1) * P].bitcast(FP8X4),
                     lhsT_scale=w2_scales[:, g, h * P : (h + 1) * P],
-                    rhs=rq[unit, g][:].bitcast(FP8X4),
-                    rhs_scale=rs[unit, g][:],
+                    rhs=r_codes[2 * n + g][:].bitcast(FP8X4),
+                    rhs_scale=r_scales[2 * n + g][:],
                     start=(g == 0),
                     stop=(g == PASSES - 1),
                 )
 
-        def add_bias2(unit, h, on_vector):
-            y[unit, h] = work.tile([P, unit[2] * P], F32, name="y", bufs=6)
-            if on_vector:
-                nc.vector.tensor_scalar(
-                    out=y[unit, h][:], in0=y_ps[unit, h][:], scalar1=b2_col[:, h : h + 1], scalar2=None, op0=ALU.add
-                )
-            else:
-                nc.scalar.activation(
-                    out=y[unit, h][:], in_=y_ps[unit, h][:], func=ACT.Identity, bias=b2_col[:, h : h + 1]
-                )
+        def add_b2(m):
+            y[m] = work.tile([P, GROUP], F32, name="y", bufs=6)
+            nc.scalar.activation(out=y[m][:], in_=y_ps[m][:], func=ACT.Identity, bias=b2_col[:, m % 2 : m % 2 + 1])
 
-        def pool_nodes(unit, h):
+        def pool_nodes(m):
+            n, h = divmod(m, 2)
             if h == 0:
-                pooled[unit] = work.tile([P, HALVES * POLYS, 1], F32, name="pooled", bufs=3)
+                pooled[n] = work.tile([P, HALVES * POLYS, 1], F32, name="pooled", bufs=3)
             nc.vector.tensor_reduce(
-                out=pooled[unit][:, h * POLYS : (h + 1) * POLYS, 0],
-                in_=y[unit, h][:].rearrange("p (j b q) -> p b j q", j=unit[2], b=POLYS),
+                out=pooled[n][:, h * POLYS : (h + 1) * POLYS, 0],
+                in_=y[m][:].rearrange("p (j b q) -> p b j q", j=TILES_PER_GROUP, b=POLYS),
                 axis=mybir.AxisListType.XY,
                 op=ALU.max,
             )
 
-        def spread_pooled(unit, other=None):
-            wide = [P, HALVES * POLYS, ROWS_PER_POLY]
-            spread[unit] = work.tile(wide, F32, name="spread", bufs=2)
-            if other is None:
-                nc.vector.tensor_copy(out=spread[unit][:], in_=pooled[unit][:].to_broadcast(wide))
-            else:
-                nc.vector.tensor_tensor(
-                    out=spread[unit][:],
-                    in0=pooled[unit][:].to_broadcast(wide),
-                    in1=pooled[other][:].to_broadcast(wide),
-                    op=ALU.max,
-                )
-
-        def turn_y(unit, h, bank="ring"):
-            yt[unit, h] = psum.tile([P, unit[2], P], F32, name=bank, bufs=3)
-            for j in range(unit[2]):
-                nc.tensor.transpose(yt[unit, h][:, j, :], y[unit, h][:, j * P : (j + 1) * P], ident[:])
-
-        def store_own(unit, h, engine_copy):
+        def store_own(m):
+            n, h = divmod(m, 2)
+            own_ps[m] = psum_tile([P, TILES_PER_GROUP, P], "ring")
+            for j in range(TILES_PER_GROUP):
+                nc.tensor.transpose(own_ps[m][:, j, :], y[m][:, j * P : (j + 1) * P], ident[:])
             if h == 0:
-                own[unit] = work.tile([P, TILES_PER_GROUP, G], F32, name="own", bufs=2)
-            engine_copy(out=own[unit][:, :, h * P : (h + 1) * P], in_=yt[unit, h][:])
+                own[n] = work.tile([P, TILES_PER_GROUP, G], F32, name="own", bufs=2)
+            nc.scalar.copy(out=own[n][:, :, h * P : (h + 1) * P], in_=own_ps[m][:])
             if h == HALVES - 1:
-                nc.sync.dma_start(out=out_rows[unit[0], :, :, 0:G], in_=own[unit][:])
+                nc.sync.dma_start(out=out_rows[n, :, :, 0:G], in_=own[n][:])
 
-        def turn_pooled(unit, bank="ring"):
-            yt[unit, 2] = psum.tile([P, 1, G], F32, name=bank, bufs=3)
-            flat = spread[unit][:].rearrange("p a q -> p (a q)")
+        def spread_pooled(n):
+            wide = [P, HALVES * POLYS, ROWS_PER_POLY]
+            spread[n] = work.tile(wide, F32, name="spread", bufs=2)
+            nc.vector.tensor_copy(out=spread[n][:], in_=pooled[n][:].to_broadcast(wide))
+
+        def store_pooled(n, bank, engine_copy):
+            pooled_ps[n] = psum_tile([P, 1, G], bank)
+            flat = spread[n][:].rearrange("p a q -> p (a q)")
             for h in range(HALVES):
-                nc.tensor.transpose(yt[unit, 2][:, 0, h * P : (h + 1) * P], flat[:, h * P : (h + 1) * P], ident[:])
+                nc.tensor.transpose(pooled_ps[n][:, 0, h * P : (h + 1) * P], flat[:, h * P : (h + 1) * P], ident[:])
+            shared = work.tile([P, 1, G], F32, name="shared", bufs=3)
+            engine_copy(out=shared[:], in_=pooled_ps[n][:])
+            nc.sync.dma_start(out=out_rows[n, :, :, G : 2 * G], in_=shared[:].to_broadcast([P, TILES_PER_GROUP, G]))
 
-        def store_pooled(unit, engine_copy):
-            shared[unit] = work.tile([P, 1, G], F32, name="shared", bufs=3)
-            engine_copy(out=shared[unit][:], in_=yt[unit, 2][:])
-            nc.sync.dma_start(
-                out=out_rows[unit[0], :, :, G : 2 * G], in_=shared[unit][:].to_broadcast([P, TILES_PER_GROUP, G])
-            )
-
-        def whole(k):
-            return (k, 0, TILES_PER_GROUP)
-
-        def on_tile(stage, i, *args):
+        def on_tile(step, i, *args):
             if 0 <= i < TILES:
-                stage(i, *args)
+                step(i, *args)
 
-        def on_half(stage, n, *args):
-            k, half = divmod(n, 2)
-            if 0 <= k < GROUPS:
-                stage(whole(k), half, *args)
+        def on_half(step, m, *args):
+            if m >= 0:
+                step(m, *args)
 
-        def plane(n, t, bank="ring", bufs=3):
-            k, g = divmod(n, 2)
-            if 0 <= k < GROUPS:
-                turn_n(whole(k), PACK * g + t, bank, bufs)
+        def on_group(step, m, *args):
+            if m >= 0 and m % 2 == 0:
+                step(m // 2, *args)
 
-        def relu(n, t, on_vector=False):
-            k, g = divmod(n, 2)
-            if 0 <= k < GROUPS:
-                affine_relu(whole(k), PACK * g + t, on_vector)
-
-        def on_group(stage, n, *args):
-            k, half = divmod(n, 2)
-            if half == 0 and 0 <= k < GROUPS:
-                stage(whole(k), *args)
-
-        def prepare_x(i):
+        def scale_and_turn_x(i):
             scale_x(i, 0)
             scale_x(i, 1)
             turn_x(i)
 
-        prepare_x(0)
+        scale_and_turn_x(0)
         group_w1(0, 0, nc.scalar.copy, 0, PACK)
-        prepare_x(1)
-        copy_x(0)
-        copy_x(1)
+        scale_and_turn_x(1)
+        copy_x(0, nc.scalar.copy)
+        copy_x(1, nc.scalar.copy)
         group_w1(1, 0, nc.vector.tensor_copy, 0, PACK)
-        prepare_x(2)
+        scale_and_turn_x(2)
         quantize_w1(0, 0)
         quantize_x(0)
         quantize_w1(1, 0)
         matmul1(0, 0)
         group_w1(0, 1, nc.scalar.copy, 0, PACK)
-        group_w1(1, 1, nc.scalar.copy, 0, W_SHARE)
-        prepare_x(3)
-        group_w1(1, 1, nc.vector.tensor_copy, W_SHARE, PACK)
+        group_w1(1, 1, nc.scalar.copy, 0, PACK // 2)
+        scale_and_turn_x(3)
+        group_w1(1, 1, nc.vector.tensor_copy, PACK // 2, PACK)
         quantize_w1(0, 1)
         prepare_b1()
-        copy_x(2)
-        copy_x(3)
+        copy_x(2, nc.scalar.copy)
+        copy_x(3, nc.scalar.copy)
         quantize_w1(1, 1)
         scale_x(4, 0)
         scale_x(4, 1)
@@ -462,184 +446,177 @@ def tile_sub_graph_pa_t_kernel(tc, x_bytes, x_scale, w1, b1, gamma, beta, w2, b2
         matmul1(1, 0)
         quantize_x(2)
 
-        for q in range(PAIRS - 2):
+        for q in range(PAIRS - TURN_LEAD // 2):
             even, odd = 2 * q, 2 * q + 1
-            pool_share, scalar_share = POOL_SHARE, 0
-            if q < 6:
-                pool_share, scalar_share = FIRST_POOL_SHARE, FIRST_SCALAR_SHARE
-            if odd + 5 >= TILES:
-                pool_share = LAST_POOL_SHARE
+            with_outputs = q >= OUT_LAG
+            x_on_vector = with_outputs and q % 2 == 0
+            if not with_outputs or odd + SCALE_LEAD >= TILES:
+                pool_share = POOL_SHARE_SHORT
+            elif x_on_vector:
+                pool_share = POOL_SHARE_LONG
+            else:
+                pool_share = POOL_SHARE
+            vector_first = pool_share if with_outputs else pool_share + SCALAR_SHARE
 
-            on_tile(inverse, even - 2)
             on_tile(normalize, even - 2, nc.gpsimd)
-            on_half(group_r, q - 4, nc.gpsimd, 0, pool_share)
-            on_tile(turn_x, even + 4)
-            plane(q - 3, 0)
-            on_tile(add_bias, even)
+            on_half(group_r_gpsimd, q - QUANT_LAG, 0, pool_share)
+            turn_x(even + TURN_LEAD)
+            on_half(turn_plane, q - PLANE_LAG, 0, "ring")
+            add_b1(even, 0)
+            if x_on_vector:
+                copy_x(even + TURN_LEAD, nc.vector.tensor_copy)
+            add_b1(even, 1)
             on_tile(variance, even - 1)
-            on_tile(copy_x, even + 4)
-            on_tile(deviation, even - 1)
-            relu(q - 3, 0)
-            on_tile(matmul1, odd, 1)
-            on_tile(scale_x, even + 5, 0)
-            on_tile(mean, even)
-            on_tile(scale_x, even + 5, 1)
-            plane(q - 3, 1)
-            relu(q - 3, 1)
-            on_group(turn_pooled, q - 8)
-            on_group(store_pooled, q - 8, nc.scalar.copy)
-            on_tile(matmul1, even + 2, 0)
+            if x_on_vector:
+                relu_plane(q - PLANE_LAG, 0)
+                deviation(even - 1)
+            else:
+                copy_x(even + TURN_LEAD, nc.scalar.copy)
+                on_tile(deviation, even - 1)
+                on_half(relu_plane, q - PLANE_LAG, 0)
+            matmul1(odd, 1)
+            scale_x(even + SCALE_LEAD, 0)
+            mean(even)
+            scale_x(even + SCALE_LEAD, 1)
+            on_half(turn_plane, q - PLANE_LAG, 1, "ring")
+            on_half(relu_plane, q - PLANE_LAG, 1)
+            on_group(store_pooled, q - POOLED_LAG, "ring", nc.scalar.copy)
+            matmul1(even + 2, 0)
             if q == 0:
                 prepare_columns()
-            if q == W2_A:
                 group_w2(0)
-            if q == W2_B:
+            if q == PLANE_LAG - 1:
                 group_w2(1)
 
-            on_half(matmul2, q - 6)
-            on_tile(inverse, odd - 2)
+            on_half(matmul2, q - OUT_LAG, "ring")
             on_tile(normalize, odd - 2, nc.gpsimd)
-            on_tile(turn_x, odd + 4)
-            on_tile(add_bias, odd)
-            on_half(add_bias2, q - 6, False)
-            on_tile(variance, odd - 1)
-            plane(q - 3, 2)
-            on_tile(copy_x, odd + 4)
-            on_tile(deviation, odd - 1)
-            on_half(group_r, q - 4, nc.scalar, pool_share, pool_share + scalar_share)
-            relu(q - 3, 2)
-            on_tile(matmul1, even + 2, 1)
-            on_tile(scale_x, odd + 5, 0)
-            on_tile(mean, odd)
-            on_tile(scale_x, odd + 5, 1)
-            plane(q - 3, 3)
-            relu(q - 3, 3)
-            on_half(turn_y, q - 6)
-            on_half(store_own, q - 6, nc.scalar.copy)
-            on_tile(matmul1, odd + 2, 0)
-            on_half(pool_nodes, q - 6)
-            on_half(group_r, q - 4, nc.vector, pool_share + scalar_share, GROUP)
-            on_tile(quantize_x, even + 4)
-            on_group(spread_pooled, q - 7)
-            on_half(quantize_r, q - 4)
-            if q == W2_B + 1:
+            turn_x(odd + TURN_LEAD)
+            add_b1(odd, 0)
+            add_b1(odd, 1)
+            on_half(add_b2, q - OUT_LAG)
+            variance(even)
+            on_half(turn_plane, q - PLANE_LAG, 2, "ring")
+            copy_x(odd + TURN_LEAD, nc.scalar.copy)
+            deviation(even)
+            if not with_outputs:
+                on_half(group_r_scalar, q - QUANT_LAG, pool_share, vector_first)
+            on_half(relu_plane, q - PLANE_LAG, 2)
+            matmul1(even + 2, 1)
+            on_tile(scale_x, odd + SCALE_LEAD, 0)
+            mean(odd)
+            on_tile(scale_x, odd + SCALE_LEAD, 1)
+            on_half(turn_plane, q - PLANE_LAG, 3, "ring")
+            on_half(relu_plane, q - PLANE_LAG, 3)
+            on_half(store_own, q - OUT_LAG)
+            matmul1(odd + 2, 0)
+            on_half(pool_nodes, q - OUT_LAG)
+            on_half(group_r_vector, q - QUANT_LAG, vector_first, GROUP)
+            quantize_x(even + TURN_LEAD)
+            on_group(spread_pooled, q - SPREAD_LAG)
+            on_half(quantize_r, q - QUANT_LAG)
+            if q == PLANE_LAG:
                 quantize_w2()
 
-        for q in range(PAIRS - 2, PAIRS):
+        for q in range(PAIRS - TURN_LEAD // 2, PAIRS):
             even, odd = 2 * q, 2 * q + 1
-            inverse(even - 2)
             normalize(even - 2, nc.gpsimd)
-            on_half(group_r, q - 4, nc.gpsimd, 0, END_SHARE)
-            plane(q - 3, 0, "scale0", 1)
-            on_half(matmul2, q - 6)
-            add_bias(even)
+            group_r_gpsimd(q - QUANT_LAG, 0, POOL_SHARE_SHORT)
+            turn_plane(q - PLANE_LAG, 0, "scale0")
+            matmul2(q - OUT_LAG, "ring")
+            add_b1(even, 0)
+            add_b1(even, 1)
             variance(even - 1)
-            on_half(add_bias2, q - 6, False)
+            add_b2(q - OUT_LAG)
             deviation(even - 1)
             matmul1(odd, 1)
-            plane(q - 3, 1)
-            plane(q - 3, 2, "scale1", 1)
-            relu(q - 3, 0, True)
+            turn_plane(q - PLANE_LAG, 1, "ring")
+            turn_plane(q - PLANE_LAG, 2, "scale1")
+            affine_plane(q - PLANE_LAG, 0)
             mean(even)
-            relu(q - 3, 1)
+            relu_plane(q - PLANE_LAG, 1)
             variance(even)
             on_tile(matmul1, even + 2, 0)
-            inverse(odd - 2)
             normalize(odd - 2, nc.gpsimd)
-            add_bias(odd)
-            plane(q - 3, 3)
-            relu(q - 3, 3)
+            add_b1(odd, 0)
+            add_b1(odd, 1)
+            turn_plane(q - PLANE_LAG, 3, "ring")
+            relu_plane(q - PLANE_LAG, 3)
             deviation(even)
-            on_half(turn_y, q - 6)
-            on_half(store_own, q - 6, nc.scalar.copy)
-            on_group(turn_pooled, q - 8)
-            on_group(store_pooled, q - 8, nc.scalar.copy)
+            store_own(q - OUT_LAG)
+            on_group(store_pooled, q - POOLED_LAG, "ring", nc.scalar.copy)
             on_tile(matmul1, even + 2, 1)
             on_tile(matmul1, odd + 2, 0)
-            relu(q - 3, 2, True)
+            affine_plane(q - PLANE_LAG, 2)
             mean(odd)
-            on_half(pool_nodes, q - 6)
-            on_half(group_r, q - 4, nc.vector, END_SHARE, GROUP)
-            on_group(spread_pooled, q - 7)
-            on_half(quantize_r, q - 4)
+            pool_nodes(q - OUT_LAG)
+            group_r_vector(q - QUANT_LAG, POOL_SHARE_SHORT, GROUP)
+            on_group(spread_pooled, q - SPREAD_LAG)
+            quantize_r(q - QUANT_LAG)
 
-        last = TILES - 1
-        k4, k5, k6, k7 = (whole(k) for k in range(GROUPS - 4, GROUPS))
+        last_tile = TILES - 1
+        group_a, group_b, group_c = GROUPS - 3, GROUPS - 2, GROUPS - 1
+        a_lo, a_hi, b_lo, b_hi, c_lo, c_hi = range(2 * group_a, 2 * GROUPS)
 
-        def own_store(unit, h, bank):
-            turn_y(unit, h, bank)
-            store_own(unit, h, nc.scalar.copy)
+        def relu_planes(m, steps):
+            for t in steps:
+                turn_plane(m, t, "ring")
+                relu_plane(m, t)
 
-        def pooled_store(unit, bank, engine_copy):
-            turn_pooled(unit, bank)
-            store_pooled(unit, engine_copy)
-
-        variance(last)
-        plane(13, 0)
-        plane(13, 1)
-        relu(13, 0)
-        deviation(last)
-        inverse(last - 1)
-        normalize(last - 1, nc.vector)
-        inverse(last)
-        normalize(last, nc.vector)
-        plane(13, 2)
-        plane(13, 3, "scale0", 1)
-        relu(13, 1)
-        pooled_store(k4, "hps", nc.scalar.copy)
-        relu(13, 2)
-        matmul2(k5, 0, "hps")
-        add_bias2(k5, 0, False)
-        group_r(k6, 0, nc.vector, 0, GROUP)
-        relu(13, 3, True)
-        group_r(k6, 1, nc.gpsimd, 0, T2)
-        pool_nodes(k5, 0)
-        for t in range(PACK):
-            if t % 2 == 1 and VT > t // 2:
-                plane(14, t, "scale%d" % (1 - t // 2), 1)
-                relu(14, t, True)
-            else:
-                plane(14, t)
-                relu(14, t)
-        matmul2(k5, 1, "hps")
-        add_bias2(k5, 1, False)
-        for t in range(PACK):
-            if t % 2 == 1 and VT > 2 + t // 2:
-                plane(15, t, "scale%d" % (t // 2), 1)
-                relu(15, t, True)
-            else:
-                plane(15, t)
-                relu(15, t)
-        pool_nodes(k5, 1)
-        group_r(k6, 1, nc.vector, T2, GROUP)
-        quantize_r(k6, 0)
-        quantize_r(k6, 1)
-        group_r(k7, 0, nc.vector, 0, GROUP)
-        own_store(k5, 0, "ring")
-        own_store(k5, 1, "ring")
-        matmul2(k6, 0, "hps")
-        group_r(k7, 1, nc.scalar, 0, T3)
-        add_bias2(k6, 0, False)
-        matmul2(k6, 1, "hps")
-        add_bias2(k6, 1, False)
-        spread_pooled(k5)
-        quantize_r(k7, 0)
-        group_r(k7, 1, nc.vector, T3, GROUP)
-        pooled_store(k5, "ring", nc.scalar.copy)
-        quantize_r(k7, 1)
-        own_store(k6, 0, "ring")
-        own_store(k6, 1, "ring")
-        pool_nodes(k6, 0)
-        pool_nodes(k6, 1)
-        matmul2(k7, 0, "hps")
-        matmul2(k7, 1, "hps")
-        add_bias2(k7, 0, False)
-        add_bias2(k7, 1, False)
-        spread_pooled(k6)
-        pool_nodes(k7, 0)
-        pool_nodes(k7, 1)
-        pooled_store(k6, "ring", nc.scalar.copy)
-        own_store(k7, 0, "ring")
-        spread_pooled(k7)
-        own_store(k7, 1, "ring")
-        pooled_store(k7, "hps", nc.vector.tensor_copy)
+        variance(last_tile)
+        turn_plane(b_hi, 0, "ring")
+        turn_plane(b_hi, 1, "ring")
+        relu_plane(b_hi, 0)
+        deviation(last_tile)
+        normalize(last_tile - 1, nc.vector)
+        normalize(last_tile, nc.vector)
+        turn_plane(b_hi, 2, "ring")
+        turn_plane(b_hi, 3, "scale0")
+        relu_plane(b_hi, 1)
+        store_pooled(group_a - 1, "h", nc.scalar.copy)
+        relu_plane(b_hi, 2)
+        matmul2(a_lo, "h")
+        add_b2(a_lo)
+        group_r_vector(b_lo, 0, GROUP)
+        affine_plane(b_hi, 3)
+        group_r_gpsimd(b_hi, 0, POOL_SHARE)
+        pool_nodes(a_lo)
+        relu_planes(c_lo, [0])
+        turn_plane(c_lo, 1, "scale1")
+        affine_plane(c_lo, 1)
+        relu_planes(c_lo, [2, 3])
+        matmul2(a_hi, "h")
+        add_b2(a_hi)
+        relu_planes(c_hi, range(PACK))
+        pool_nodes(a_hi)
+        group_r_vector(b_hi, POOL_SHARE, GROUP)
+        quantize_r(b_lo)
+        quantize_r(b_hi)
+        group_r_vector(c_lo, 0, GROUP)
+        store_own(a_lo)
+        store_own(a_hi)
+        matmul2(b_lo, "h")
+        group_r_scalar(c_hi, 0, SCALAR_SHARE)
+        add_b2(b_lo)
+        matmul2(b_hi, "h")
+        add_b2(b_hi)
+        spread_pooled(group_a)
+        quantize_r(c_lo)
+        group_r_vector(c_hi, SCALAR_SHARE, GROUP)
+        store_pooled(group_a, "ring", nc.scalar.copy)
+        quantize_r(c_hi)
+        store_own(b_lo)
+        store_own(b_hi)
+        pool_nodes(b_lo)
+        pool_nodes(b_hi)
+        matmul2(c_lo, "h")
+        matmul2(c_hi, "h")
+        add_b2(c_lo)
+        add_b2(c_hi)
+        spread_pooled(group_b)
+        pool_nodes(c_lo)
+        pool_nodes(c_hi)
+        store_pooled(group_b, "ring", nc.scalar.copy)
+        store_own(c_lo)
+        spread_pooled(group_c)
+        store_own(c_hi)
+        store_pooled(group_c, "h", nc.vector.tensor_copy)

@@ -42,8 +42,7 @@ POOLED_LAG = 8
 SCALE_LEAD = 5
 TURN_LEAD = 4
 
-POOL_SHARE = 320
-POOL_SHARE_LONG = 384
+POOL_SHARE = 352
 POOL_SHARE_SHORT = 192
 SCALAR_SHARE = 128
 
@@ -90,10 +89,10 @@ def tile_sub_graph_pa_t_kernel(tc, x_bytes, x_scale, w1, b1, gamma, beta, w2, b2
         load_w1(0, 0)
         load_w1(1, 0)
         load_x(2, 2)
+        b1_raw = keep.tile([P, PASSES, PACK], BF16)
+        nc.sync.dma_start(out=b1_raw[:], in_=b1.rearrange("(c p t) -> p c t", p=P, t=PACK))
         load_w1(0, 1)
         load_w1(1, 1)
-        b1_raw = keep.tile([P, H], BF16)
-        nc.sync.dma_start(out=b1_raw[:], in_=b1.partition_broadcast(P))
         load_x(TILES_PER_GROUP, TILES_PER_GROUP)
         gamma_raw = keep.tile([P, PASSES, PACK], BF16)
         nc.sync.dma_start(out=gamma_raw[:], in_=gamma.rearrange("(g p t) -> p g t", p=P, t=PACK))
@@ -136,7 +135,9 @@ def tile_sub_graph_pa_t_kernel(tc, x_bytes, x_scale, w1, b1, gamma, beta, w2, b2
                 in_=w1_grouped[g, c][:].rearrange("p t m j -> p (t m j)"),
             )
 
+        b1_col = keep.tile([P, PASSES, PACK], F32)
         b1_row = keep.tile([P, PASSES, PACK, P], F32)
+        b1_turned = {}
         gamma_col = keep.tile([P, PASSES, PACK], F32)
         beta_col = keep.tile([P, PASSES, PACK], F32)
         b2_col = keep.tile([P, HALVES], F32)
@@ -144,8 +145,16 @@ def tile_sub_graph_pa_t_kernel(tc, x_bytes, x_scale, w1, b1, gamma, beta, w2, b2
         w2_codes = keep.tile([P, PASSES, G], U32, align_bytes=64)
         w2_scales = keep.tile([P, PASSES, G], U8, align_bytes=64)
 
-        def prepare_b1():
-            nc.scalar.copy(out=b1_row[:], in_=b1_raw[:].rearrange("p (c m t) -> p c t m", c=PASSES, t=PACK))
+        def turn_b1():
+            nc.scalar.copy(out=b1_col[:], in_=b1_raw[:])
+            for c in range(PASSES):
+                b1_turned[c] = psum_tile([P, PACK, P], "h")
+                for t in range(PACK):
+                    nc.tensor.transpose(b1_turned[c][:, t, :], b1_col[:, c, t : t + 1].to_broadcast([P, P]), ident[:])
+
+        def copy_b1():
+            for c in range(PASSES):
+                nc.scalar.copy(out=b1_row[:, c, :, :], in_=b1_turned[c][:])
 
         def prepare_columns():
             nc.scalar.copy(out=gamma_col[:], in_=gamma_raw[:])
@@ -187,11 +196,11 @@ def tile_sub_graph_pa_t_kernel(tc, x_bytes, x_scale, w1, b1, gamma, beta, w2, b2
                     every_second = words[:, 2 * P * g + u : 2 * P * (g + 1) : 2]
                     nc.tensor.transpose(x_turned[i][:, g, u, :], every_second, ident[:])
 
-        def copy_x(i, engine_copy):
+        def copy_x(i):
             pair, place = divmod(i, 2)
             if place == 0:
                 x_grouped[pair] = work.tile([P, 2, H], BF16, name="x_grouped", bufs=2, align_bytes=64)
-            engine_copy(
+            nc.scalar.copy(
                 out=x_grouped[pair][:, place, :].bitcast(F32).rearrange("p (g r u) -> p g r u", g=PASSES, u=2),
                 in_=x_turned[i][:].rearrange("p g u r -> p g r u"),
             )
@@ -423,8 +432,9 @@ def tile_sub_graph_pa_t_kernel(tc, x_bytes, x_scale, w1, b1, gamma, beta, w2, b2
         scale_and_turn_x(0)
         group_w1(0, 0, nc.scalar.copy, 0, PACK)
         scale_and_turn_x(1)
-        copy_x(0, nc.scalar.copy)
-        copy_x(1, nc.scalar.copy)
+        copy_x(0)
+        copy_x(1)
+        turn_b1()
         group_w1(1, 0, nc.vector.tensor_copy, 0, PACK)
         scale_and_turn_x(2)
         quantize_w1(0, 0)
@@ -436,9 +446,9 @@ def tile_sub_graph_pa_t_kernel(tc, x_bytes, x_scale, w1, b1, gamma, beta, w2, b2
         scale_and_turn_x(3)
         group_w1(1, 1, nc.vector.tensor_copy, PACK // 2, PACK)
         quantize_w1(0, 1)
-        prepare_b1()
-        copy_x(2, nc.scalar.copy)
-        copy_x(3, nc.scalar.copy)
+        copy_b1()
+        copy_x(2)
+        copy_x(3)
         quantize_w1(1, 1)
         scale_x(4, 0)
         scale_x(4, 1)
@@ -449,13 +459,7 @@ def tile_sub_graph_pa_t_kernel(tc, x_bytes, x_scale, w1, b1, gamma, beta, w2, b2
         for q in range(PAIRS - TURN_LEAD // 2):
             even, odd = 2 * q, 2 * q + 1
             with_outputs = q >= OUT_LAG
-            x_on_vector = with_outputs and q % 2 == 0
-            if not with_outputs or odd + SCALE_LEAD >= TILES:
-                pool_share = POOL_SHARE_SHORT
-            elif x_on_vector:
-                pool_share = POOL_SHARE_LONG
-            else:
-                pool_share = POOL_SHARE
+            pool_share = POOL_SHARE if with_outputs and odd + SCALE_LEAD < TILES else POOL_SHARE_SHORT
             vector_first = pool_share if with_outputs else pool_share + SCALAR_SHARE
 
             on_tile(normalize, even - 2, nc.gpsimd)
@@ -463,17 +467,11 @@ def tile_sub_graph_pa_t_kernel(tc, x_bytes, x_scale, w1, b1, gamma, beta, w2, b2
             turn_x(even + TURN_LEAD)
             on_half(turn_plane, q - PLANE_LAG, 0, "ring")
             add_b1(even, 0)
-            if x_on_vector:
-                copy_x(even + TURN_LEAD, nc.vector.tensor_copy)
             add_b1(even, 1)
             on_tile(variance, even - 1)
-            if x_on_vector:
-                relu_plane(q - PLANE_LAG, 0)
-                deviation(even - 1)
-            else:
-                copy_x(even + TURN_LEAD, nc.scalar.copy)
-                on_tile(deviation, even - 1)
-                on_half(relu_plane, q - PLANE_LAG, 0)
+            copy_x(even + TURN_LEAD)
+            on_tile(deviation, even - 1)
+            on_half(relu_plane, q - PLANE_LAG, 0)
             matmul1(odd, 1)
             scale_x(even + SCALE_LEAD, 0)
             mean(even)
@@ -496,7 +494,7 @@ def tile_sub_graph_pa_t_kernel(tc, x_bytes, x_scale, w1, b1, gamma, beta, w2, b2
             on_half(add_b2, q - OUT_LAG)
             variance(even)
             on_half(turn_plane, q - PLANE_LAG, 2, "ring")
-            copy_x(odd + TURN_LEAD, nc.scalar.copy)
+            copy_x(odd + TURN_LEAD)
             deviation(even)
             if not with_outputs:
                 on_half(group_r_scalar, q - QUANT_LAG, pool_share, vector_first)

from contextlib import ExitStack

import concourse.mybir as mybir
from concourse.masks import make_identity

B, L, H, G = 64, 64, 1024, 256
EPS = 1e-5
FLOPS = 2 * B * L * H * (H + G)

F32 = mybir.dt.float32
BF16 = mybir.dt.bfloat16
U32 = mybir.dt.uint32
U8 = mybir.dt.uint8
FP8 = mybir.dt.float8_e4m3fn
FP8X4 = mybir.dt.float8_e4m3fn_x4
ALU = mybir.AluOpType
ACT = mybir.ActivationFunctionType

P = 128
PACK = 4
K_PASS = P * PACK
PASSES = H // K_PASS
BANK = 512
TILES_PER_GROUP = 4
GROUP = P * TILES_PER_GROUP
GROUPS = B * L // GROUP
TILES = GROUPS * TILES_PER_GROUP
PAIRS = TILES // 2
HALVES = G // P
POLYS = GROUP // L
ROWS_PER_POLY = P // POLYS
BF16_MAX = 3.3895313892515355e38

H_BANKS = 3
RING_BANKS = 3

PLANE_LAG = 3
QUANT_LAG = 4
OUT_LAG = 6
SPREAD_LAG = 7
POOLED_LAG = 8
SCALE_LEAD = 5
TURN_LEAD = 4

POOL_SHARE = 352
POOL_SHARE_SHORT = 192
SCALAR_SHARE = 128


def tile_sub_graph_pa_t_kernel(tc, x_bytes, x_scale, w1, b1, gamma, beta, w2, b2, out):
    nc = tc.nc
    x_rows = x_bytes.rearrange("b l h -> (b l) h").rearrange("(n p j) h -> n p j h", p=P, j=TILES_PER_GROUP)
    out_rows = out.rearrange("b l c -> (b l) c").rearrange("(n p j) c -> n p j c", p=P, j=TILES_PER_GROUP)

    with ExitStack() as ctx:
        keep = ctx.enter_context(tc.tile_pool(name="keep", bufs=1))
        work = ctx.enter_context(tc.tile_pool(name="work", bufs=2))
        psum = ctx.enter_context(tc.psum_pool(name="psum", bufs=1))
        ctx.enter_context(tc.manual_schedule())

        bank_bufs = {"scale0": 1, "scale1": 1, "h": H_BANKS, "ring": RING_BANKS}

        def psum_tile(shape, bank):
            return psum.tile(shape, F32, name=bank, bufs=bank_bufs[bank])

        ident = keep.tile([P, P], F32)
        make_identity(nc, ident[:])

        scale_col = keep.tile([P, PASSES, PACK], F32)
        nc.sync.dma_start(out=scale_col[:], in_=x_scale.rearrange("a b (g p t) -> p (a b g) t", p=P, t=PACK))

        xb = {}

        def load_x(first, count):
            n, j = divmod(first, TILES_PER_GROUP)
            rows = keep.tile([P, count, H], U8, name="xbytes%d" % first)
            nc.sync.dma_start(out=rows[:], in_=x_rows[n, :, j : j + count, :])
            for step in range(count):
                xb[first + step] = rows[:, step, :]

        w1_raw = {}

        def load_w1(g, c):
            w1_raw[g, c] = keep.tile([P, PACK, BANK], BF16, name="w1raw%d%d" % (g, c))
            rows = w1[g * K_PASS : (g + 1) * K_PASS, c * BANK : (c + 1) * BANK]
            nc.sync.dma_start(out=w1_raw[g, c][:], in_=rows.rearrange("(p j) n -> p j n", j=PACK))

        load_x(0, 2)
        load_w1(0, 0)
        load_w1(1, 0)
        load_x(2, 2)
        b1_raw = keep.tile([P, PASSES, PACK], BF16)
        nc.sync.dma_start(out=b1_raw[:], in_=b1.rearrange("(c p t) -> p c t", p=P, t=PACK))
        load_w1(0, 1)
        load_w1(1, 1)
        load_x(TILES_PER_GROUP, TILES_PER_GROUP)
        gamma_raw = keep.tile([P, PASSES, PACK], BF16)
        nc.sync.dma_start(out=gamma_raw[:], in_=gamma.rearrange("(g p t) -> p g t", p=P, t=PACK))
        beta_raw = keep.tile([P, PASSES, PACK], BF16)
        nc.sync.dma_start(out=beta_raw[:], in_=beta.rearrange("(g p t) -> p g t", p=P, t=PACK))
        w2_raw = keep.tile([P, PASSES, PACK, G], BF16)
        nc.sync.dma_start(
            out=w2_raw[:].rearrange("p g j n -> p g (j n)"),
            in_=w2.rearrange("(g p j) n -> p g (j n)", p=P, j=PACK),
        )
        b2_raw = keep.tile([P, HALVES, 2], BF16)
        with nc.allow_non_contiguous_dma(reason="one bias value to a partition and half"):
            nc.sync.dma_start(out=b2_raw[:, :, 0], in_=b2.rearrange("(h p) -> p h", p=P))
        for n in range(2, GROUPS):
            load_x(n * TILES_PER_GROUP, TILES_PER_GROUP)

        scale_row = []
        for g in range(PASSES):
            bank = psum_tile([P, P, PACK], "scale%d" % g)
            for t in range(PACK):
                nc.tensor.transpose(bank[:, :, t], scale_col[:, g, t : t + 1].to_broadcast([P, P]), ident[:])
            scale_row.append(bank)

        w1_grouped, w1_codes, w1_scales = {}, {}, {}

        def group_w1(g, c, engine_copy, first, last):
            if (g, c) not in w1_grouped:
                w1_grouped[g, c] = keep.tile([P, PACK, P, PACK], BF16, name="w1grp%d%d" % (g, c), align_bytes=64)
            engine_copy(
                out=w1_grouped[g, c][:, first:last, :, :].rearrange("p t (a i) j -> p a t i j", i=2),
                in_=w1_raw[g, c][:].rearrange("p j (a i t) -> p a t i j", i=2, t=PACK)[:, :, first:last, :, :],
            )

        def quantize_w1(g, c):
            w1_codes[g, c] = keep.tile([P, BANK], U32, name="w1codes%d%d" % (g, c), align_bytes=64)
            w1_scales[g, c] = keep.tile([P, BANK], U8, name="w1scales%d%d" % (g, c), align_bytes=64)
            nc.vector.quantize_mx(
                out=w1_codes[g, c][:].bitcast(FP8X4),
                scales=w1_scales[g, c][:],
                in_=w1_grouped[g, c][:].rearrange("p t m j -> p (t m j)"),
            )

        b1_col = keep.tile([P, PASSES, PACK], F32)
        b1_row = keep.tile([P, PASSES, PACK, P], F32)
        b1_turned = {}
        gamma_col = keep.tile([P, PASSES, PACK], F32)
        beta_col = keep.tile([P, PASSES, PACK], F32)
        b2_col = keep.tile([P, HALVES], F32)
        w2_grouped = keep.tile([P, PASSES, G, PACK], BF16, align_bytes=64)
        w2_codes = keep.tile([P, PASSES, G], U32, align_bytes=64)
        w2_scales = keep.tile([P, PASSES, G], U8, align_bytes=64)

        def turn_b1():
            nc.scalar.copy(out=b1_col[:], in_=b1_raw[:])
            for c in range(PASSES):
                b1_turned[c] = psum_tile([P, PACK, P], "h")
                for t in range(PACK):
                    nc.tensor.transpose(b1_turned[c][:, t, :], b1_col[:, c, t : t + 1].to_broadcast([P, P]), ident[:])

        def copy_b1():
            for c in range(PASSES):
                nc.scalar.copy(out=b1_row[:, c, :, :], in_=b1_turned[c][:])

        def prepare_columns():
            nc.scalar.copy(out=gamma_col[:], in_=gamma_raw[:])
            nc.scalar.copy(out=beta_col[:], in_=beta_raw[:])
            nc.scalar.copy(out=b2_col[:], in_=b2_raw[:, :, 0])

        def group_w2(g):
            nc.scalar.copy(
                out=w2_grouped[:, g, :, :].rearrange("p (a i) j -> p a j i", i=4),
                in_=w2_raw[:, g, :, :].rearrange("p j (a i) -> p a j i", i=4),
            )

        def quantize_w2():
            nc.vector.quantize_mx(
                out=w2_codes[:].rearrange("p g n -> p (g n)").bitcast(FP8X4),
                scales=w2_scales[:].rearrange("p g n -> p (g n)"),
                in_=w2_grouped[:].rearrange("p g n j -> p (g n j)"),
            )

        x_wide, x_turned, x_grouped, x_codes, x_scales = {}, {}, {}, {}, {}
        h_ps, hb, sums, neg_mean, sum_sq, std, rstd, normed = {}, {}, {}, {}, {}, {}, {}, {}

        def scale_x(i, g):
            if g == 0:
                x_wide[i] = work.tile([P, H], BF16, name="x_wide", bufs=3)
            cols = slice(g * K_PASS, (g + 1) * K_PASS)
            nc.vector.tensor_tensor(
                out=x_wide[i][:, cols],
                in0=xb[i][:, cols].bitcast(FP8),
                in1=scale_row[g][:].rearrange("p m t -> p (m t)"),
                op=ALU.mult,
            )

        def turn_x(i):
            x_turned[i] = psum_tile([P, PASSES, 2, P], "ring")
            words = x_wide[i][:].bitcast(F32)
            for g in range(PASSES):
                for u in range(2):
                    every_second = words[:, 2 * P * g + u : 2 * P * (g + 1) : 2]
                    nc.tensor.transpose(x_turned[i][:, g, u, :], every_second, ident[:])

        def copy_x(i):
            pair, place = divmod(i, 2)
            if place == 0:
                x_grouped[pair] = work.tile([P, 2, H], BF16, name="x_grouped", bufs=2, align_bytes=64)
            nc.scalar.copy(
                out=x_grouped[pair][:, place, :].bitcast(F32).rearrange("p (g r u) -> p g r u", g=PASSES, u=2),
                in_=x_turned[i][:].rearrange("p g u r -> p g r u"),
            )

        def quantize_x(i):
            codes = work.tile([P, 2, PASSES, P], U32, name="x_codes", bufs=3, align_bytes=64)
            scales = work.tile([P, 2, PASSES, P], U8, name="x_scales", bufs=3, align_bytes=64)
            nc.vector.quantize_mx(
                out=codes[:].rearrange("p n g r -> p (n g r)").bitcast(FP8X4),
                scales=scales[:].rearrange("p n g r -> p (n g r)"),
                in_=x_grouped[i // 2][:].rearrange("p n c -> p (n c)"),
            )
            for place in range(2):
                x_codes[i + place] = codes[:, place, :, :]
                x_scales[i + place] = scales[:, place, :, :]

        def matmul1(i, c):
            h_ps[i, c] = psum_tile([P, BANK], "h")
            for g in range(PASSES):
                nc.tensor.matmul_mx(
                    out=h_ps[i, c][:],
                    lhsT=x_codes[i][:, g, :].bitcast(FP8X4),
                    lhsT_scale=x_scales[i][:, g, :],
                    rhs=w1_codes[g, c][:].bitcast(FP8X4),
                    rhs_scale=w1_scales[g, c][:],
                    start=(g == 0),
                    stop=(g == PASSES - 1),
                )

        def add_b1(i, c):
            if c == 0:
                hb[i] = work.tile([P, PASSES, BANK], F32, name="hb", bufs=4)
                sums[i] = work.tile([P, PASSES], F32, name="sums", bufs=3)
            nc.vector.scalar_tensor_tensor(
                out=hb[i][:, c, :],
                in0=h_ps[i, c][:],
                scalar=1.0,
                in1=b1_row[:, c, :, :].rearrange("p t m -> p (t m)"),
                op0=ALU.mult,
                op1=ALU.add,
                accum_out=sums[i][:, c : c + 1],
            )

        def mean(i):
            neg_mean[i] = work.tile([P, 1], F32, name="neg_mean", bufs=4)
            nc.vector.tensor_scalar(
                out=neg_mean[i][:],
                in0=sums[i][:, 0:1],
                scalar1=sums[i][:, 1:2],
                scalar2=-1.0 / H,
                op0=ALU.add,
                op1=ALU.mult,
            )

        def variance(i):
            squares = work.tile([P, H], BF16, name="squares", bufs=2)
            sum_sq[i] = work.tile([P, 1], F32, name="sum_sq", bufs=3)
            nc.scalar.activation(
                out=squares[:],
                in_=hb[i][:].rearrange("p c n -> p (c n)"),
                func=ACT.Square,
                bias=neg_mean[i][:],
                accum_out=sum_sq[i][:],
            )

        def deviation(i):
            std[i] = work.tile([P, 1], F32, name="std", bufs=3)
            nc.scalar.activation(out=std[i][:], in_=sum_sq[i][:], func=ACT.Sqrt, scale=1.0 / H, bias=EPS)

        def normalize(i, engine):
            rstd[i] = work.tile([P, 1], F32, name="rstd", bufs=3)
            nc.vector.reciprocal(out=rstd[i][:], in_=std[i][:])
            normed[i] = work.tile([P, H], F32, name="normed", bufs=8)
            engine.tensor_scalar(
                out=normed[i][:],
                in0=hb[i][:].rearrange("p c n -> p (c n)"),
                scalar1=neg_mean[i][:],
                scalar2=rstd[i][:],
                op0=ALU.add,
                op1=ALU.mult,
            )

        n_turned, planes, r_grouped, r_codes, r_scales = {}, {}, {}, {}, {}
        y_ps, y, pooled, spread, own_ps, own, pooled_ps = {}, {}, {}, {}, {}, {}, {}

        def turn_plane(m, t, bank):
            n, g = divmod(m, 2)
            first = g * BANK + t * P
            n_turned[m, t] = psum_tile([P, TILES_PER_GROUP, P], bank)
            for j in range(TILES_PER_GROUP):
                rows = normed[n * TILES_PER_GROUP + j]
                nc.tensor.transpose(n_turned[m, t][:, j, :], rows[:, first : first + P], ident[:])

        def plane_out(m, t):
            if m not in planes:
                planes[m] = work.tile([P, PACK, GROUP], BF16, name="planes", bufs=4)
            return planes[m][:, t, :]

        def relu_plane(m, t):
            nc.scalar.activation(
                out=plane_out(m, t),
                in_=n_turned[m, t][:].rearrange("p j r -> p (j r)"),
                func=ACT.Relu,
                scale=gamma_col[:, m % 2, t : t + 1],
                bias=beta_col[:, m % 2, t : t + 1],
            )

        def affine_plane(m, t):
            nc.vector.tensor_scalar(
                out=plane_out(m, t),
                in0=n_turned[m, t][:].rearrange("p j r -> p (j r)"),
                scalar1=gamma_col[:, m % 2, t : t + 1],
                scalar2=beta_col[:, m % 2, t : t + 1],
                op0=ALU.mult,
                op1=ALU.add,
            )

        def group_out(m):
            if m not in r_grouped:
                r_grouped[m] = work.tile([P, GROUP, PACK], BF16, name="r_grouped", bufs=3, align_bytes=64)
            return r_grouped[m]

        def group_r_gpsimd(m, first, last):
            nc.gpsimd.tensor_scalar(
                out=group_out(m)[:, first:last, :],
                in0=planes[m][:, :, first:last].rearrange("p t n -> p n t"),
                scalar1=BF16_MAX,
                scalar2=0.0,
                op0=ALU.min,
                op1=ALU.max,
            )

        def group_r_vector(m, first, last):
            nc.vector.tensor_scalar(
                out=group_out(m)[:, first:last, :].rearrange("p (a i) t -> p a t i", i=4),
                in0=planes[m][:, :, first:last].rearrange("p t (a i) -> p a t i", i=4),
                scalar1=BF16_MAX,
                scalar2=0.0,
                op0=ALU.min,
                op1=ALU.max,
            )

        def group_r_scalar(m, first, last):
            nc.scalar.copy(
                out=group_out(m)[:, first:last, :].rearrange("p (a i) t -> p a t i", i=4),
                in_=planes[m][:, :, first:last].rearrange("p t (a i) -> p a t i", i=4),
            )

        def quantize_r(m):
            r_codes[m] = work.tile([P, GROUP], U32, name="r_codes", bufs=4, align_bytes=64)
            r_scales[m] = work.tile([P, GROUP], U8, name="r_scales", bufs=4, align_bytes=64)
            nc.vector.quantize_mx(
                out=r_codes[m][:].bitcast(FP8X4),
                scales=r_scales[m][:],
                in_=r_grouped[m][:].rearrange("p n t -> p (n t)"),
            )

        def matmul2(m, bank):
            n, h = divmod(m, 2)
            y_ps[m] = psum_tile([P, GROUP], bank)
            for g in range(PASSES):
                nc.tensor.matmul_mx(
                    out=y_ps[m][:],
                    lhsT=w2_codes[:, g, h * P : (h + 1) * P].bitcast(FP8X4),
                    lhsT_scale=w2_scales[:, g, h * P : (h + 1) * P],
                    rhs=r_codes[2 * n + g][:].bitcast(FP8X4),
                    rhs_scale=r_scales[2 * n + g][:],
                    start=(g == 0),
                    stop=(g == PASSES - 1),
                )

        def add_b2(m):
            y[m] = work.tile([P, GROUP], F32, name="y", bufs=6)
            nc.scalar.activation(out=y[m][:], in_=y_ps[m][:], func=ACT.Identity, bias=b2_col[:, m % 2 : m % 2 + 1])

        def pool_nodes(m):
            n, h = divmod(m, 2)
            if h == 0:
                pooled[n] = work.tile([P, HALVES * POLYS, 1], F32, name="pooled", bufs=3)
            nc.vector.tensor_reduce(
                out=pooled[n][:, h * POLYS : (h + 1) * POLYS, 0],
                in_=y[m][:].rearrange("p (j b q) -> p b j q", j=TILES_PER_GROUP, b=POLYS),
                axis=mybir.AxisListType.XY,
                op=ALU.max,
            )

        def store_own(m):
            n, h = divmod(m, 2)
            own_ps[m] = psum_tile([P, TILES_PER_GROUP, P], "ring")
            for j in range(TILES_PER_GROUP):
                nc.tensor.transpose(own_ps[m][:, j, :], y[m][:, j * P : (j + 1) * P], ident[:])
            if h == 0:
                own[n] = work.tile([P, TILES_PER_GROUP, G], F32, name="own", bufs=2)
            nc.scalar.copy(out=own[n][:, :, h * P : (h + 1) * P], in_=own_ps[m][:])
            if h == HALVES - 1:
                nc.sync.dma_start(out=out_rows[n, :, :, 0:G], in_=own[n][:])

        def spread_pooled(n):
            wide = [P, HALVES * POLYS, ROWS_PER_POLY]
            spread[n] = work.tile(wide, F32, name="spread", bufs=2)
            nc.vector.tensor_copy(out=spread[n][:], in_=pooled[n][:].to_broadcast(wide))

        def store_pooled(n, bank, engine_copy):
            pooled_ps[n] = psum_tile([P, 1, G], bank)
            flat = spread[n][:].rearrange("p a q -> p (a q)")
            for h in range(HALVES):
                nc.tensor.transpose(pooled_ps[n][:, 0, h * P : (h + 1) * P], flat[:, h * P : (h + 1) * P], ident[:])
            shared = work.tile([P, 1, G], F32, name="shared", bufs=3)
            engine_copy(out=shared[:], in_=pooled_ps[n][:])
            nc.sync.dma_start(out=out_rows[n, :, :, G : 2 * G], in_=shared[:].to_broadcast([P, TILES_PER_GROUP, G]))

        def on_tile(step, i, *args):
            if 0 <= i < TILES:
                step(i, *args)

        def on_half(step, m, *args):
            if m >= 0:
                step(m, *args)

        def on_group(step, m, *args):
            if m >= 0 and m % 2 == 0:
                step(m // 2, *args)

        def scale_and_turn_x(i):
            scale_x(i, 0)
            scale_x(i, 1)
            turn_x(i)

        scale_and_turn_x(0)
        group_w1(0, 0, nc.scalar.copy, 0, PACK)
        scale_and_turn_x(1)
        copy_x(0)
        copy_x(1)
        turn_b1()
        group_w1(1, 0, nc.vector.tensor_copy, 0, PACK)
        scale_and_turn_x(2)
        quantize_w1(0, 0)
        quantize_x(0)
        quantize_w1(1, 0)
        matmul1(0, 0)
        group_w1(0, 1, nc.scalar.copy, 0, PACK)
        group_w1(1, 1, nc.scalar.copy, 0, PACK // 2)
        scale_and_turn_x(3)
        group_w1(1, 1, nc.vector.tensor_copy, PACK // 2, PACK)
        quantize_w1(0, 1)
        copy_b1()
        copy_x(2)
        copy_x(3)
        quantize_w1(1, 1)
        scale_x(4, 0)
        scale_x(4, 1)
        matmul1(0, 1)
        matmul1(1, 0)
        quantize_x(2)

        for q in range(PAIRS - TURN_LEAD // 2):
            even, odd = 2 * q, 2 * q + 1
            with_outputs = q >= OUT_LAG
            pool_share = POOL_SHARE if with_outputs and odd + SCALE_LEAD < TILES else POOL_SHARE_SHORT
            vector_first = pool_share if with_outputs else pool_share + SCALAR_SHARE

            on_tile(normalize, even - 2, nc.gpsimd)
            on_half(group_r_gpsimd, q - QUANT_LAG, 0, pool_share)
            turn_x(even + TURN_LEAD)
            on_half(turn_plane, q - PLANE_LAG, 0, "ring")
            add_b1(even, 0)
            add_b1(even, 1)
            on_tile(variance, even - 1)
            copy_x(even + TURN_LEAD)
            on_tile(deviation, even - 1)
            on_half(relu_plane, q - PLANE_LAG, 0)
            matmul1(odd, 1)
            scale_x(even + SCALE_LEAD, 0)
            mean(even)
            scale_x(even + SCALE_LEAD, 1)
            on_half(turn_plane, q - PLANE_LAG, 1, "ring")
            on_half(relu_plane, q - PLANE_LAG, 1)
            on_group(store_pooled, q - POOLED_LAG, "ring", nc.scalar.copy)
            matmul1(even + 2, 0)
            if q == 0:
                prepare_columns()
                group_w2(0)
            if q == PLANE_LAG - 1:
                group_w2(1)

            on_half(matmul2, q - OUT_LAG, "ring")
            on_tile(normalize, odd - 2, nc.gpsimd)
            turn_x(odd + TURN_LEAD)
            add_b1(odd, 0)
            add_b1(odd, 1)
            on_half(add_b2, q - OUT_LAG)
            variance(even)
            on_half(turn_plane, q - PLANE_LAG, 2, "ring")
            copy_x(odd + TURN_LEAD)
            deviation(even)
            if not with_outputs:
                on_half(group_r_scalar, q - QUANT_LAG, pool_share, vector_first)
            on_half(relu_plane, q - PLANE_LAG, 2)
            matmul1(even + 2, 1)
            on_tile(scale_x, odd + SCALE_LEAD, 0)
            mean(odd)
            on_tile(scale_x, odd + SCALE_LEAD, 1)
            on_half(turn_plane, q - PLANE_LAG, 3, "ring")
            on_half(relu_plane, q - PLANE_LAG, 3)
            on_half(store_own, q - OUT_LAG)
            matmul1(odd + 2, 0)
            on_half(pool_nodes, q - OUT_LAG)
            on_half(group_r_vector, q - QUANT_LAG, vector_first, GROUP)
            quantize_x(even + TURN_LEAD)
            on_group(spread_pooled, q - SPREAD_LAG)
            on_half(quantize_r, q - QUANT_LAG)
            if q == PLANE_LAG:
                quantize_w2()

        for q in range(PAIRS - TURN_LEAD // 2, PAIRS):
            even, odd = 2 * q, 2 * q + 1
            normalize(even - 2, nc.gpsimd)
            group_r_gpsimd(q - QUANT_LAG, 0, POOL_SHARE_SHORT)
            turn_plane(q - PLANE_LAG, 0, "scale0")
            matmul2(q - OUT_LAG, "ring")
            add_b1(even, 0)
            add_b1(even, 1)
            variance(even - 1)
            add_b2(q - OUT_LAG)
            deviation(even - 1)
            matmul1(odd, 1)
            turn_plane(q - PLANE_LAG, 1, "ring")
            turn_plane(q - PLANE_LAG, 2, "scale1")
            affine_plane(q - PLANE_LAG, 0)
            mean(even)
            relu_plane(q - PLANE_LAG, 1)
            variance(even)
            on_tile(matmul1, even + 2, 0)
            normalize(odd - 2, nc.gpsimd)
            add_b1(odd, 0)
            add_b1(odd, 1)
            turn_plane(q - PLANE_LAG, 3, "ring")
            relu_plane(q - PLANE_LAG, 3)
            deviation(even)
            store_own(q - OUT_LAG)
            on_group(store_pooled, q - POOLED_LAG, "ring", nc.scalar.copy)
            on_tile(matmul1, even + 2, 1)
            on_tile(matmul1, odd + 2, 0)
            affine_plane(q - PLANE_LAG, 2)
            mean(odd)
            pool_nodes(q - OUT_LAG)
            group_r_vector(q - QUANT_LAG, POOL_SHARE_SHORT, GROUP)
            on_group(spread_pooled, q - SPREAD_LAG)
            quantize_r(q - QUANT_LAG)

        last_tile = TILES - 1
        group_a, group_b, group_c = GROUPS - 3, GROUPS - 2, GROUPS - 1
        a_lo, a_hi, b_lo, b_hi, c_lo, c_hi = range(2 * group_a, 2 * GROUPS)

        def relu_planes(m, steps):
            for t in steps:
                turn_plane(m, t, "ring")
                relu_plane(m, t)

        variance(last_tile)
        turn_plane(b_hi, 0, "ring")
        turn_plane(b_hi, 1, "ring")
        relu_plane(b_hi, 0)
        deviation(last_tile)
        normalize(last_tile - 1, nc.vector)
        normalize(last_tile, nc.vector)
        turn_plane(b_hi, 2, "ring")
        turn_plane(b_hi, 3, "scale0")
        relu_plane(b_hi, 1)
        store_pooled(group_a - 1, "h", nc.scalar.copy)
        relu_plane(b_hi, 2)
        matmul2(a_lo, "h")
        add_b2(a_lo)
        group_r_vector(b_lo, 0, GROUP)
        affine_plane(b_hi, 3)
        group_r_gpsimd(b_hi, 0, POOL_SHARE)
        pool_nodes(a_lo)
        relu_planes(c_lo, [0])
        turn_plane(c_lo, 1, "scale1")
        affine_plane(c_lo, 1)
        relu_planes(c_lo, [2, 3])
        matmul2(a_hi, "h")
        add_b2(a_hi)
        relu_planes(c_hi, range(PACK))
        pool_nodes(a_hi)
        group_r_vector(b_hi, POOL_SHARE, GROUP)
        quantize_r(b_lo)
        quantize_r(b_hi)
        group_r_vector(c_lo, 0, GROUP)
        store_own(a_lo)
        store_own(a_hi)
        matmul2(b_lo, "h")
        group_r_scalar(c_hi, 0, SCALAR_SHARE)
        add_b2(b_lo)
        matmul2(b_hi, "h")
        add_b2(b_hi)
        spread_pooled(group_a)
        quantize_r(c_lo)
        group_r_vector(c_hi, SCALAR_SHARE, GROUP)
        store_pooled(group_a, "ring", nc.scalar.copy)
        quantize_r(c_hi)
        store_own(b_lo)
        store_own(b_hi)
        pool_nodes(b_lo)
        pool_nodes(b_hi)
        matmul2(c_lo, "h")
        matmul2(c_hi, "h")
        add_b2(c_lo)
        add_b2(c_hi)
        spread_pooled(group_b)
        pool_nodes(c_lo)
        pool_nodes(c_hi)
        store_pooled(group_b, "ring", nc.scalar.copy)
        store_own(c_lo)
        spread_pooled(group_c)
        store_own(c_hi)
        store_pooled(group_c, "h", nc.vector.tensor_copy)
